import numpy as np
import ml_dtypes


def mxq(x, axis, fmt="e4m3"):
    dtype, down = {"e4m3": (ml_dtypes.float8_e4m3fn, 7), "e5m2": (ml_dtypes.float8_e5m2, 14)}[fmt]
    v = np.moveaxis(np.asarray(x, np.float32).astype(ml_dtypes.bfloat16).astype(np.float64), axis, -1)
    blocks = v.reshape(v.shape[:-1] + (-1, 32))
    amax = np.abs(blocks).max(-1, keepdims=True)
    byte = np.maximum(np.where(amax > 0, np.frexp(amax)[1] - 1 + 127, 0) - down, 1)
    scale = np.exp2(byte - 127.0)
    codes = (blocks / scale).astype(np.float32).astype(dtype).astype(np.float64)
    return np.moveaxis((codes * scale).reshape(v.shape), -1, axis)


WIDE = False


def mx_kscale(k):
    if not WIDE:
        return np.ones(k)
    levels = np.array([10, -10, 5, -5, 0])
    if k % 512:
        return np.exp2(np.random.permutation(np.resize(levels, k // 32))).repeat(32)
    a = np.empty((k // 512, 16))
    for p in range(k // 512):
        a[p, :8] = np.random.permutation(np.resize(levels, 8))
        for g in range(8):
            far = levels[np.abs(levels - a[p, g]) >= 10]
            a[p, g + 8] = far[np.random.randint(len(far))]
    return np.exp2(a.ravel()).repeat(32)


BF16 = ml_dtypes.bfloat16


def bf(x):
    return np.asarray(x, np.float32).astype(BF16)


def f64(x):
    return np.asarray(x).astype(np.float64)


B, N, D, H, L, C = 16, 512, 512, 8, 3, 2
HD = D // H


def setup_inputs():
    s, t = mx_kscale(D), mx_kscale(D)
    tk = t.reshape(H, HD)[:, :L]
    return {
        "fields": bf((np.random.standard_normal((B, N, D)) + np.random.standard_normal((B, 1, D))) * t),
        "h2": bf(np.maximum(np.random.standard_normal((B, N, D)), 0.0) * 1.4 * s),
        "corr_kernels": bf(np.random.standard_normal((H, L, L)) * 2.5 / tk[:, None, :]),
        "w3": bf(np.random.standard_normal((D, D)) * 1.5 / np.sqrt(D) * t[:, None] / s[None, :]),
        "b3": bf(np.random.standard_normal(D) * 0.3 * t),
        "out_w": bf(np.random.standard_normal((D, D)) / np.sqrt(D) / t[None, :]),
        "out_b": bf(np.random.standard_normal(D) * 0.3),
        "inter_w": bf(1.0 + 0.5 * np.random.standard_normal(C)),
    }


def reference(fields, h2, corr_kernels, w3, b3, out_w, out_b, inter_w):
    f = f64(fields).reshape(B, N, H, HD)
    ck = f64(corr_kernels)
    corr = np.zeros((B, N, H, HD))
    for lag in range(1, L + 1):
        base = f[:, :-lag]
        shifted = f[:, lag:]
        w = np.pad(ck[:, lag - 1, :], ((0, 0), (0, HD - L)))
        mean_shift = shifted.mean(axis=1, keepdims=True)
        cw = base * w[None, None] * mean_shift
        corr = corr + np.pad(cw, ((0, 0), (0, lag), (0, 0), (0, 0)))
    corr = corr / L
    nl = ((mxq(f64(h2), 2, "e4m3") @ mxq(f64(w3), 1, "e4m3").T) + f64(b3)).reshape(B, N, H, HD)
    r = f64(inter_w)
    e = np.exp(r - r.max())
    iw = e / e.sum()
    enhanced = (f + iw[0] * corr + iw[1] * nl).reshape(B, N, D)
    return (mxq(enhanced, 2, "e4m3") @ mxq(f64(out_w), 1, "e4m3").T) + f64(out_b)

@@ -1,0 +1,458 @@
+from contextlib import ExitStack
+
+import concourse.mybir as mybir
+from concourse.masks import make_identity
+
+F32 = mybir.dt.float32
+BF16 = mybir.dt.bfloat16
+U32 = mybir.dt.uint32
+U8 = mybir.dt.uint8
+FP8X4 = mybir.dt.float8_e4m3fn_x4
+ALU = mybir.AluOpType
+ACT = mybir.ActivationFunctionType
+AXIS = mybir.AxisListType
+
+P = 128
+QUADRANT = 32
+BANK = 512
+B = 16
+N = 512
+D = 512
+HEADS = 8
+LAGS = 3
+STREAMS = 2
+TILES = N // P
+PLANES = 4
+WORD = 2
+HALVES = PLANES // WORD
+ROW_WORDS = D // WORD
+ROW = TILES * D
+BLOCKS_IN_BANK = BANK // (HALVES * P)
+
+KERNEL_CHANNELS = PLANES
+HEAD_PARTITIONS = P // HEADS
+SUMS = HEADS * KERNEL_CHANNELS
+SLOTS = HEADS + LAGS + 1
+FIELD_SCALES = TILES * PLANES
+TERMS = (TILES - 1) * PLANES * SLOTS
+
+PRELOADED = 3
+LOADS_AHEAD = 4
+H_AHEAD = 2
+FIELDS_AHEAD = 1
+SECOND_PRODUCT_BEHIND = 2
+FIRST_STEP = -H_AHEAD
+OUT_TILES_ON_SCALAR = 2
+WORK_BUFFERS = 2
+RESULT_BUFFERS = 3
+BANKS_IN_RUN = 2
+WORD_BANKS = 3
+PRODUCT_BANKS = 4
+TOTAL_BANKS = 1
+
+FLOPS = 2 * 2 * B * N * D * D
+
+
+def tile_fieldinteractionoperators_pa_t_kernel(
+    tc, fields, h2, corr_kernels, w3, b3, out_w, out_b, inter_w, out
+):
+    nc = tc.nc
+    with ExitStack() as ctx:
+        ctx.enter_context(tc.manual_schedule())
+        const = ctx.enter_context(tc.tile_pool(name="const", bufs=1))
+        rows_in = ctx.enter_context(tc.tile_pool(name="rows_in", bufs=LOADS_AHEAD))
+        work = ctx.enter_context(tc.tile_pool(name="work", bufs=WORK_BUFFERS))
+        rows_out = ctx.enter_context(tc.tile_pool(name="rows_out", bufs=RESULT_BUFFERS))
+        transposed = ctx.enter_context(tc.psum_pool(name="transposed", bufs=WORD_BANKS))
+        products = ctx.enter_context(tc.psum_pool(name="products", bufs=PRODUCT_BANKS))
+        totals = ctx.enter_context(tc.psum_pool(name="totals", bufs=TOTAL_BANKS))
+
+        identity = const.tile([P, P], F32)
+        make_identity(nc, identity[:])
+        terms_all = const.tile([P, B * TERMS], F32)
+        nc.gpsimd.memset(terms_all[:], 0.0)
+
+        zero_column = const.tile([P, 1], F32)
+        nc.vector.memset(zero_column[:], 0.0)
+        edge_rows = const.tile([P, ROW], BF16)
+        nc.vector.memset(edge_rows[QUADRANT : 2 * QUADRANT, :], 0.0)
+        nc.vector.memset(edge_rows[2 * QUADRANT : P, :], 0.0)
+        out_b_rows = const.tile([P, D], BF16)
+        nc.vector.memset(out_b_rows[:], 0.0)
+        ones = const.tile([P, P], BF16)
+        nc.vector.memset(ones[:], 1.0)
+        scales_all = const.tile([P, B * FIELD_SCALES], F32)
+        nc.vector.memset(scales_all[:], 1.0)
+        weights = const.tile([P, (LAGS + 2) * SUMS], F32)
+        nc.vector.memset(weights[:], 0.0)
+
+        logits = const.tile([P, STREAMS], BF16)
+        nc.sync.dma_start(out=logits[:], in_=inter_w.partition_broadcast(P))
+        kernels = const.tile([P, HEADS * LAGS * LAGS], BF16)
+        nc.sync.dma_start(out=kernels[:], in_=corr_kernels.rearrange("h l j -> (h l j)").partition_broadcast(P))
+        nc.sync.dma_start(out=edge_rows[0:B, :], in_=fields[:, 0:TILES, :].rearrange("b n c -> b (n c)"))
+        nc.sync.dma_start(out=edge_rows[B : 2 * B, :], in_=fields[:, N - TILES : N, :].rearrange("b n c -> b (n c)"))
+        nc.sync.dma_start(out=out_b_rows[0:1, :], in_=out_b.rearrange("(o c) -> o c", o=1))
+        b3_planes = const.tile([P, PLANES], BF16)
+        nc.sync.dma_start(
+            out=b3_planes[:],
+            in_=b3.rearrange("(q t) -> q t", t=PLANES),
+        )
+
+        w3_rows = const.tile([P, ROW], BF16)
+        nc.sync.dma_start(
+            out=w3_rows[:],
+            in_=w3.rearrange("(m t) k -> m (t k)", t=PLANES),
+        )
+
+        h_rows = {}
+        f_rows = {}
+
+        def load(b):
+            h_tile = rows_in.tile([P, ROW], BF16, tag="h_rows")
+            nc.sync.dma_start(out=h_tile[:], in_=h2[b].rearrange("(p i) c -> p (i c)", i=TILES))
+            h_rows[b] = h_tile
+            f_tile = rows_in.tile([P, ROW], BF16, tag="f_rows")
+            nc.sync.dma_start(out=f_tile[:], in_=fields[b].rearrange("(p i) c -> p (i c)", i=TILES))
+            f_rows[b] = f_tile
+
+        for b in range(PRELOADED):
+            load(b)
+        out_w_rows = const.tile([P, ROW], BF16)
+        nc.sync.dma_start(
+            out=out_w_rows[:].rearrange("m (a k) -> m a k", a=TILES),
+            in_=out_w.rearrange("(a m) k -> m a k", a=TILES),
+        )
+
+        def rows_to_words(rows, grouped, pair):
+            words = rows[:].bitcast(F32)
+            grouped_words = grouped[:].bitcast(F32)
+            bank = transposed.tile([P, BANK], F32, tag="words")
+            for k in range(BLOCKS_IN_BANK):
+                for u in range(HALVES):
+                    row = (BLOCKS_IN_BANK * pair + k) * ROW_WORDS
+                    nc.tensor.transpose(
+                        bank[:, (HALVES * k + u) * P : (HALVES * k + u + 1) * P],
+                        words[:, row + u : row + ROW_WORDS : HALVES],
+                        identity[:],
+                    )
+            nc.scalar.copy(
+                out=grouped_words[:, pair * BANK : (pair + 1) * BANK].rearrange(
+                    "q (k r u) -> q k r u", k=BLOCKS_IN_BANK, u=HALVES
+                ),
+                in_=bank[:].rearrange("q (k u r) -> q k r u", k=BLOCKS_IN_BANK, u=HALVES),
+            )
+
+        def quantise(grouped, codes, scales):
+            nc.vector.quantize_mx(out=codes[:].bitcast(FP8X4), scales=scales[:], in_=grouped[:])
+
+        def weight_to_words(rows):
+            grouped = work.tile([P, PLANES * D], BF16, tag="weight_grouped", bufs=1, align_bytes=64)
+            for pair in range(TILES // BLOCKS_IN_BANK):
+                rows_to_words(rows, grouped, pair)
+            return grouped
+
+
+        norm = const.tile([P, LAGS * SUMS], F32)
+        lives_here = identity[:].rearrange("p (h x) -> p h x", x=HEAD_PARTITIONS)[:, :, 0:1]
+        for lag in range(1, LAGS + 1):
+            nc.vector.tensor_scalar_mul(
+                out=norm[:, (lag - 1) * SUMS : lag * SUMS].rearrange("p (h j) -> p h j", h=HEADS),
+                in0=lives_here.to_broadcast([P, HEADS, KERNEL_CHANNELS]),
+                scalar1=1.0 / (LAGS * (N - lag)),
+            )
+
+        warm = const.tile([P, 1], F32)
+        nc.scalar.activation(out=warm[:], in_=zero_column[:], func=ACT.Exp)
+
+        own = weights[:, 2 * SUMS :]
+        nc.vector.tensor_tensor(
+            out=own.rearrange("p (l h j) -> p l h j", l=LAGS, h=HEADS)[:, :, :, 0:LAGS],
+            in0=kernels[:].rearrange("p (h l j) -> p l h j", h=HEADS, l=LAGS),
+            in1=norm[:].rearrange("p (l h j) -> p l h j", l=LAGS, h=HEADS)[:, :, :, 0:LAGS],
+            op=ALU.mult,
+        )
+        top = const.tile([P, 1], F32)
+        nc.vector.tensor_tensor(out=top[:], in0=logits[:, 0:1], in1=logits[:, 1:2], op=ALU.max)
+        minus_top = const.tile([P, 1], F32)
+        nc.vector.tensor_scalar_mul(out=minus_top[:], in0=top[:], scalar1=-1.0)
+        exps = const.tile([P, STREAMS], F32)
+        exp_sum = const.tile([P, 1], F32)
+        nc.scalar.activation(
+            out=exps[:], in_=logits[:], func=ACT.Exp, bias=minus_top[:, 0:1], scale=1.0, accum_out=exp_sum[:, 0:1]
+        )
+        for lag in range(2, LAGS + 1):
+            block = LAGS - lag
+            nc.vector.tensor_tensor(
+                out=weights[:, block * SUMS : (block + 1) * SUMS],
+                in0=weights[:, (block + 1) * SUMS : (block + 2) * SUMS],
+                in1=weights[:, (lag + 1) * SUMS : (lag + 2) * SUMS],
+                op=ALU.add,
+            )
+        plane_weight = const.tile([P, LAGS * PLANES], F32)
+        nc.vector.tensor_reduce(
+            out=plane_weight[:].rearrange("p (l t) -> p l t", t=PLANES),
+            in_=own.rearrange("p (l h t) -> p l t h", l=LAGS, h=HEADS),
+            axis=AXIS.X,
+            op=ALU.add,
+        )
+
+        heads = const.tile([P, B * LAGS * PLANES], F32)
+        last_tokens = const.tile([P, B * FIELD_SCALES], F32)
+        edge_words = edge_rows[:].bitcast(F32)
+        for u in range(HALVES):
+            edge_bank = transposed.tile([P, BANK], F32, tag="words")
+            for n in range(TILES):
+                row = n * ROW_WORDS
+                nc.tensor.transpose(
+                    edge_bank[:, n * P : (n + 1) * P], edge_words[:, row + u : row + ROW_WORDS : HALVES], identity[:]
+                )
+            edge_values = edge_bank[:].bitcast(BF16).rearrange("q (n c e) -> q n c e", n=TILES, e=WORD)
+            nc.vector.tensor_copy(
+                out=heads[:].rearrange("q (b n u e) -> q n b u e", b=B, u=HALVES, e=WORD)[:, :, :, u, :],
+                in_=edge_values[:, 0:LAGS, 0:B, :],
+            )
+            nc.vector.tensor_copy(
+                out=last_tokens[:].rearrange("q (b n u e) -> q n b u e", b=B, n=TILES, e=WORD)[:, :, :, u, :],
+                in_=edge_values[:, :, B : 2 * B, :],
+            )
+        heads_bnt = heads[:].rearrange("q (b n t) -> q b n t", b=B, t=PLANES)
+        for n in range(1, LAGS):
+            nc.vector.tensor_tensor(
+                out=heads_bnt[:, :, n, :], in0=heads_bnt[:, :, n, :], in1=heads_bnt[:, :, n - 1, :], op=ALU.add
+            )
+
+        inv_sum = const.tile([P, 1], F32)
+        nc.vector.reciprocal(out=inv_sum[:], in_=exp_sum[:])
+        iw = const.tile([P, STREAMS], F32)
+        nc.vector.tensor_scalar_mul(out=iw[:], in0=exps[:], scalar1=inv_sum[:, 0:1])
+        minus_iw0 = const.tile([P, 1], F32)
+        nc.vector.tensor_scalar_mul(out=minus_iw0[:], in0=iw[:, 0:1], scalar1=-1.0)
+        total_weight = const.tile([P, (TILES - 1) * SUMS], F32)
+        nc.vector.tensor_scalar_mul(out=total_weight[:], in0=weights[:, 0 : (TILES - 1) * SUMS], scalar1=iw[:, 0:1])
+        head_weight = const.tile([P, LAGS * PLANES], F32)
+        nc.vector.tensor_scalar_mul(out=head_weight[:], in0=plane_weight[:], scalar1=minus_iw0[:, 0:1])
+        nc.vector.memset(terms_all[:].rearrange("q (a m t) -> q a m t", m=SLOTS, t=PLANES)[:, :, SLOTS - 1, :], 1.0)
+        for i in range(TILES - 1):
+            counted = PLANES * (LAGS - i)
+            nc.vector.tensor_tensor(
+                out=terms_all[:].rearrange("q (b i x) -> q b i x", b=B, i=TILES - 1)[:, :, i, SUMS : SUMS + counted],
+                in0=heads[:].rearrange("q (b x) -> q b x", b=B)[:, :, 0:counted],
+                in1=head_weight[:, 0:counted].unsqueeze(1).to_broadcast([P, B, counted]),
+                op=ALU.mult,
+            )
+
+        nl_bias = const.tile([P, PLANES], F32)
+        nc.vector.tensor_scalar_mul(out=nl_bias[:], in0=b3_planes[:], scalar1=iw[:, 1:2])
+
+        w3_codes = const.tile([P, D], U32, align_bytes=64)
+        w3_scales = const.tile([P, D], U8, align_bytes=64)
+        quantise(weight_to_words(w3_rows), w3_codes, w3_scales)
+
+        out_bias_ps = products.tile([P, BANK], F32, tag="product")
+        nc.tensor.matmul(out=out_bias_ps[:], lhsT=ones[:], rhs=out_b_rows[:], start=True, stop=True)
+        out_bias = const.tile([P, D], F32)
+        nc.vector.tensor_copy(out=out_bias[:], in_=out_bias_ps[:])
+
+        h_grouped = {}
+        h_codes = {}
+        h_scales = {}
+        field_totals = {}
+        field_terms = {}
+        last_scaled = {}
+        enhanced = {}
+        e_codes = {}
+        e_scales = {}
+        results = {}
+        out_w_codes = const.tile([P, D], U32, align_bytes=64)
+        out_w_scales = const.tile([P, D], U8, align_bytes=64)
+
+        def total_fields(b):
+            total = totals.tile([P, SUMS], F32, tag="total")
+            kernel_channels = f_rows[b][:].rearrange("p (i h x) -> p i h x", i=TILES, h=HEADS)
+            for i in range(TILES):
+                nc.tensor.matmul(
+                    out=total[:].rearrange("p (h j) -> p h j", h=HEADS),
+                    lhsT=ones[:],
+                    rhs=kernel_channels[:, i, :, 0:KERNEL_CHANNELS],
+                    start=(i == 0),
+                    stop=(i == TILES - 1),
+                )
+            field_totals[b] = total
+
+        def field_scales_products(b):
+            nc.vector.tensor_tensor(
+                out=terms_all[:, b * TERMS : (b + 1) * TERMS].rearrange("q (i x) -> q i x", i=TILES - 1)[:, :, 0:SUMS],
+                in0=field_totals[b][:].unsqueeze(1).to_broadcast([P, TILES - 1, SUMS]),
+                in1=total_weight[:].rearrange("q (i x) -> q i x", i=TILES - 1),
+                op=ALU.mult,
+            )
+
+        def field_scales_sums(b):
+            nc.vector.tensor_reduce(
+                out=scales_all[:, b * FIELD_SCALES : b * FIELD_SCALES + (TILES - 1) * PLANES].rearrange(
+                    "q (i t) -> q i t", t=PLANES
+                ),
+                in_=terms_all[:, b * TERMS : (b + 1) * TERMS].rearrange("q (i m t) -> q i t m", m=SLOTS, t=PLANES),
+                axis=AXIS.X,
+                op=ALU.add,
+            )
+
+        def scale_last_rows(b):
+            scaled = work.tile([P, FIELD_SCALES], F32, tag="last_scaled")
+            nc.gpsimd.tensor_tensor(
+                out=scaled[:],
+                in0=last_tokens[:, b * FIELD_SCALES : (b + 1) * FIELD_SCALES],
+                in1=scales_all[:, b * FIELD_SCALES : (b + 1) * FIELD_SCALES],
+                op=ALU.mult,
+            )
+            last_scaled[b] = scaled
+
+        def write_last_rows(b):
+            nc.gpsimd.tensor_tensor(
+                out=field_terms[b][:].rearrange("q (t i r) -> q i t r", t=PLANES, i=TILES)[:, :, :, P - 1],
+                in0=last_scaled[b][:].rearrange("q (i t) -> q i t", i=TILES),
+                in1=nl_bias[:].unsqueeze(1).to_broadcast([P, TILES, PLANES]),
+                op=ALU.add,
+            )
+
+        def transpose_h(b, pair):
+            if pair == 0:
+                grouped = work.tile([P, PLANES * N], BF16, tag="h_grouped", align_bytes=64)
+                h_grouped[b] = grouped
+            rows_to_words(h_rows[b], h_grouped[b], pair)
+
+        def transpose_fields(b, u):
+            if u == 0:
+                term = work.tile([P, PLANES * N], F32, tag="field_term")
+                field_terms[b] = term
+            f_words = f_rows[b][:].bitcast(F32)
+            bank = transposed.tile([P, BANK], F32, tag="words")
+            for i in range(TILES):
+                row = i * ROW_WORDS
+                nc.tensor.transpose(
+                    bank[:, i * P : (i + 1) * P], f_words[:, row + u : row + ROW_WORDS : HALVES], identity[:]
+                )
+            values = bank[:].bitcast(BF16).rearrange("q (x e) -> q x e", e=WORD)
+            for e in range(WORD):
+                t = WORD * u + e
+                nc.scalar.activation(
+                    out=field_terms[b][:, t * N : (t + 1) * N],
+                    in_=values[:, :, e],
+                    func=ACT.Identity,
+                    bias=nl_bias[:, t : t + 1],
+                    scale=scales_all[:, b * FIELD_SCALES + t : b * FIELD_SCALES + t + 1],
+                )
+
+        def quantise_h(b):
+            codes = work.tile([P, N], U32, tag="h_codes", align_bytes=64)
+            scales = work.tile([P, N], U8, tag="h_scales", align_bytes=64)
+            quantise(h_grouped[b], codes, scales)
+            h_codes[b] = codes
+            h_scales[b] = scales
+
+        def first_product_and_fusion(b, i):
+            if i == 0:
+                fused = work.tile([P, PLANES * N], BF16, tag="enhanced", align_bytes=64)
+                enhanced[b] = fused
+            tokens = slice(i * P, (i + 1) * P)
+            nl = products.tile([P, BANK], F32, tag="product")
+            for t in range(PLANES):
+                channels = slice(t * P, (t + 1) * P)
+                nc.tensor.matmul_mx(
+                    out=nl[:, channels],
+                    lhsT=w3_codes[:, channels].bitcast(FP8X4),
+                    lhsT_scale=w3_scales[:, channels],
+                    rhs=h_codes[b][:, tokens].bitcast(FP8X4),
+                    rhs_scale=h_scales[b][:, tokens],
+                    start=True,
+                    stop=True,
+                )
+            nc.vector.scalar_tensor_tensor(
+                out=enhanced[b][:, i * BANK : (i + 1) * BANK].rearrange("q (r t) -> q r t", t=PLANES),
+                in0=nl[:].rearrange("q (t r) -> q r t", t=PLANES),
+                scalar=iw[:, 1:2],
+                in1=field_terms[b][:].rearrange("q (t i r) -> q i r t", t=PLANES, i=TILES)[:, i],
+                op0=ALU.mult,
+                op1=ALU.add,
+            )
+
+        def quantise_enhanced(b):
+            codes = work.tile([P, N], U32, tag="e_codes", align_bytes=64)
+            scales = work.tile([P, N], U8, tag="e_scales", align_bytes=64)
+            quantise(enhanced[b], codes, scales)
+            e_codes[b] = codes
+            e_scales[b] = scales
+
+        def second_product_and_store(b, i, on_scalar):
+            if i == 0:
+                result = rows_out.tile([P, TILES * D], F32, tag="result")
+                results[b] = result
+            tokens = slice(i * P, (i + 1) * P)
+            columns = slice(i * D, (i + 1) * D)
+            projected = products.tile([P, BANK], F32, tag="product")
+            nc.tensor.matmul_mx(
+                out=projected[:],
+                lhsT=e_codes[b][:, tokens].bitcast(FP8X4),
+                lhsT_scale=e_scales[b][:, tokens],
+                rhs=out_w_codes[:].bitcast(FP8X4),
+                rhs_scale=out_w_scales[:],
+                start=True,
+                stop=True,
+            )
+            if on_scalar:
+                nc.scalar.copy(out=results[b][:, columns], in_=projected[:])
+                nc.gpsimd.tensor_tensor(
+                    out=results[b][:, columns], in0=results[b][:, columns], in1=out_bias[:], op=ALU.add
+                )
+            else:
+                nc.vector.tensor_tensor(out=results[b][:, columns], in0=projected[:], in1=out_bias[:], op=ALU.add)
+            if i % 2 == 1:
+                half = slice((i - 1) * D, (i + 1) * D)
+                nc.sync.dma_start(out=out[b].rearrange("(p i) o -> p (i o)", i=TILES)[:, half], in_=results[b][:, half])
+
+        def entry(b):
+            return 0 <= b < B
+
+        def transpose_a_bank(j, k):
+            if k < TILES // BLOCKS_IN_BANK:
+                if entry(j + H_AHEAD):
+                    transpose_h(j + H_AHEAD, k)
+            elif entry(j + FIELDS_AHEAD):
+                transpose_fields(j + FIELDS_AHEAD, k - TILES // BLOCKS_IN_BANK)
+
+        def step(j):
+            if PRELOADED <= j + LOADS_AHEAD < B:
+                load(j + LOADS_AHEAD)
+            if entry(j + FIELDS_AHEAD):
+                field_scales_products(j + FIELDS_AHEAD)
+                quantise_h(j + FIELDS_AHEAD)
+                field_scales_sums(j + FIELDS_AHEAD)
+                scale_last_rows(j + FIELDS_AHEAD)
+            tiles_on_scalar = OUT_TILES_ON_SCALAR if entry(j) else 0
+            if entry(j - SECOND_PRODUCT_BEHIND):
+                for i in range(tiles_on_scalar):
+                    second_product_and_store(j - SECOND_PRODUCT_BEHIND, i, True)
+            for i in range(TILES):
+                if entry(j):
+                    first_product_and_fusion(j, i)
+                if (i + 1) % BANKS_IN_RUN == 0:
+                    for k in range(i + 1 - BANKS_IN_RUN, i + 1):
+                        transpose_a_bank(j, k)
+            if entry(j + FIELDS_AHEAD):
+                write_last_rows(j + FIELDS_AHEAD)
+            if entry(j - SECOND_PRODUCT_BEHIND):
+                for i in range(tiles_on_scalar, TILES):
+                    second_product_and_store(j - SECOND_PRODUCT_BEHIND, i, False)
+            if entry(j):
+                quantise_enhanced(j)
+            if entry(j + H_AHEAD):
+                total_fields(j + H_AHEAD)
+
+        for j in range(FIRST_STEP, SECOND_PRODUCT_BEHIND - 1):
+            step(j)
+        out_w_grouped = weight_to_words(out_w_rows)
+        step(SECOND_PRODUCT_BEHIND - 1)
+        quantise(out_w_grouped, out_w_codes, out_w_scales)
+        for j in range(SECOND_PRODUCT_BEHIND, B + SECOND_PRODUCT_BEHIND):
+            step(j)

@@ -13,14 +13,16 @@ ACT = mybir.ActivationFunctionType
 AXIS = mybir.AxisListType
 
 P = 128
-QUADRANT = 32
 BANK = 512
 B = 16
 N = 512
 D = 512
 HEADS = 8
+EDGE_TOKENS = 2
 LAGS = 3
+KERNELS = HEADS * LAGS * LAGS
 STREAMS = 2
+INTER_W = 80
 TILES = N // P
 PLANES = 4
 WORD = 2
@@ -29,23 +31,23 @@ ROW_WORDS = D // WORD
 ROW = TILES * D
 BLOCKS_IN_BANK = BANK // (HALVES * P)
 
-KERNEL_CHANNELS = PLANES
+KERNEL_CHANNELS = 3
 HEAD_PARTITIONS = P // HEADS
-SUMS = HEADS * KERNEL_CHANNELS
-SLOTS = HEADS + LAGS + 1
+SUMS = KERNEL_CHANNELS * HEADS
+SCALED_TILES = LAGS
+SLOTS = HEADS + 1
+BASE = HEADS
+TERMS = SCALED_TILES * KERNEL_CHANNELS * SLOTS
 FIELD_SCALES = TILES * PLANES
-TERMS = (TILES - 1) * PLANES * SLOTS
 
-PRELOADED = 3
-LOADS_AHEAD = 4
+LOADS_AHEAD = 6
 H_AHEAD = 2
 FIELDS_AHEAD = 1
-SECOND_PRODUCT_BEHIND = 2
-FIRST_STEP = -H_AHEAD
+SECOND_PRODUCT_BEHIND = 1
 OUT_TILES_ON_SCALAR = 2
+LAST_OUT_TILES_ON_SCALAR = 1
 WORK_BUFFERS = 2
 RESULT_BUFFERS = 3
-BANKS_IN_RUN = 2
 WORD_BANKS = 3
 PRODUCT_BANKS = 4
 TOTAL_BANKS = 1
@@ -70,64 +72,65 @@ def tile_fieldinteractionoperators_pa_t_kernel(
         identity = const.tile([P, P], F32)
         make_identity(nc, identity[:])
         terms_all = const.tile([P, B * TERMS], F32)
-        nc.gpsimd.memset(terms_all[:], 0.0)
 
         zero_column = const.tile([P, 1], F32)
         nc.vector.memset(zero_column[:], 0.0)
-        edge_rows = const.tile([P, ROW], BF16)
-        nc.vector.memset(edge_rows[QUADRANT : 2 * QUADRANT, :], 0.0)
-        nc.vector.memset(edge_rows[2 * QUADRANT : P, :], 0.0)
-        out_b_rows = const.tile([P, D], BF16)
-        nc.vector.memset(out_b_rows[:], 0.0)
+        vector_rows = const.tile([P, D + INTER_W + STREAMS], BF16)
+        nc.vector.memset(vector_rows[:], 0.0)
+        edge_rows = const.tile([P, EDGE_TOKENS * D], BF16)
+        nc.gpsimd.memset(edge_rows[P // 2 :, :], 0.0)
         ones = const.tile([P, P], BF16)
         nc.vector.memset(ones[:], 1.0)
         scales_all = const.tile([P, B * FIELD_SCALES], F32)
         nc.vector.memset(scales_all[:], 1.0)
         weights = const.tile([P, (LAGS + 2) * SUMS], F32)
-        nc.vector.memset(weights[:], 0.0)
-
-        logits = const.tile([P, STREAMS], BF16)
-        nc.sync.dma_start(out=logits[:], in_=inter_w.partition_broadcast(P))
-        kernels = const.tile([P, HEADS * LAGS * LAGS], BF16)
-        nc.sync.dma_start(out=kernels[:], in_=corr_kernels.rearrange("h l j -> (h l j)").partition_broadcast(P))
-        nc.sync.dma_start(out=edge_rows[0:B, :], in_=fields[:, 0:TILES, :].rearrange("b n c -> b (n c)"))
-        nc.sync.dma_start(out=edge_rows[B : 2 * B, :], in_=fields[:, N - TILES : N, :].rearrange("b n c -> b (n c)"))
-        nc.sync.dma_start(out=out_b_rows[0:1, :], in_=out_b.rearrange("(o c) -> o c", o=1))
-        b3_planes = const.tile([P, PLANES], BF16)
-        nc.sync.dma_start(
-            out=b3_planes[:],
-            in_=b3.rearrange("(q t) -> q t", t=PLANES),
-        )
-
-        w3_rows = const.tile([P, ROW], BF16)
-        nc.sync.dma_start(
-            out=w3_rows[:],
-            in_=w3.rearrange("(m t) k -> m (t k)", t=PLANES),
-        )
 
         h_rows = {}
         f_rows = {}
 
-        def load(b):
+        def load_h(b):
             h_tile = rows_in.tile([P, ROW], BF16, tag="h_rows")
             nc.sync.dma_start(out=h_tile[:], in_=h2[b].rearrange("(p i) c -> p (i c)", i=TILES))
             h_rows[b] = h_tile
+
+        def load_fields(b):
             f_tile = rows_in.tile([P, ROW], BF16, tag="f_rows")
             nc.sync.dma_start(out=f_tile[:], in_=fields[b].rearrange("(p i) c -> p (i c)", i=TILES))
             f_rows[b] = f_tile
 
-        for b in range(PRELOADED):
-            load(b)
+        for m in range(2 * TILES // EDGE_TOKENS):
+            token = EDGE_TOKENS * m if m < TILES // EDGE_TOKENS else N - 2 * TILES + EDGE_TOKENS * m
+            nc.sync.dma_start(
+                out=edge_rows[B * m : B * (m + 1), :],
+                in_=fields[:, token : token + EDGE_TOKENS, :].rearrange("b n c -> b (n c)"),
+            )
+        nc.sync.dma_start(
+            out=vector_rows[0:1, D + INTER_W : D + INTER_W + STREAMS], in_=inter_w.rearrange("(o s) -> o s", o=1)
+        )
+        nc.sync.dma_start(
+            out=vector_rows[0:1, D : D + KERNELS], in_=corr_kernels.rearrange("(o h) l j -> o (h l j)", o=1)
+        )
+        load_h(0)
+        load_fields(0)
+        w3_rows = const.tile([P, ROW], BF16)
+        nc.sync.dma_start(out=w3_rows[:], in_=w3.rearrange("(m t) k -> m (t k)", t=PLANES))
+        b3_planes = const.tile([P, PLANES], BF16)
+        nc.sync.dma_start(out=b3_planes[:], in_=b3.rearrange("(q t) -> q t", t=PLANES))
+        load_h(1)
         out_w_rows = const.tile([P, ROW], BF16)
         nc.sync.dma_start(
             out=out_w_rows[:].rearrange("m (a k) -> m a k", a=TILES),
             in_=out_w.rearrange("(a m) k -> m a k", a=TILES),
         )
+        nc.sync.dma_start(out=vector_rows[0:1, 0:D], in_=out_b.rearrange("(o c) -> o c", o=1))
+        load_fields(1)
+        for b in range(2, LOADS_AHEAD):
+            load_h(b)
+            load_fields(b)
 
-        def rows_to_words(rows, grouped, pair):
+        def rows_to_words(rows, grouped, pair, bank, copy):
             words = rows[:].bitcast(F32)
             grouped_words = grouped[:].bitcast(F32)
-            bank = transposed.tile([P, BANK], F32, tag="words")
             for k in range(BLOCKS_IN_BANK):
                 for u in range(HALVES):
                     row = (BLOCKS_IN_BANK * pair + k) * ROW_WORDS
@@ -136,7 +139,7 @@ def tile_fieldinteractionoperators_pa_t_kernel(
                         words[:, row + u : row + ROW_WORDS : HALVES],
                         identity[:],
                     )
-            nc.scalar.copy(
+            copy(
                 out=grouped_words[:, pair * BANK : (pair + 1) * BANK].rearrange(
                     "q (k r u) -> q k r u", k=BLOCKS_IN_BANK, u=HALVES
                 ),
@@ -147,41 +150,64 @@ def tile_fieldinteractionoperators_pa_t_kernel(
             nc.vector.quantize_mx(out=codes[:].bitcast(FP8X4), scales=scales[:], in_=grouped[:])
 
         def weight_to_words(rows):
-            grouped = work.tile([P, PLANES * D], BF16, tag="weight_grouped", bufs=1, align_bytes=64)
+            grouped = work.tile([P, PLANES * D], BF16, tag="weight_grouped", align_bytes=64)
             for pair in range(TILES // BLOCKS_IN_BANK):
-                rows_to_words(rows, grouped, pair)
+                bank = products.tile([P, BANK], F32, tag="product")
+                rows_to_words(rows, grouped, pair, bank, nc.vector.tensor_copy)
             return grouped
 
-
-        norm = const.tile([P, LAGS * SUMS], F32)
-        lives_here = identity[:].rearrange("p (h x) -> p h x", x=HEAD_PARTITIONS)[:, :, 0:1]
-        for lag in range(1, LAGS + 1):
-            nc.vector.tensor_scalar_mul(
-                out=norm[:, (lag - 1) * SUMS : lag * SUMS].rearrange("p (h j) -> p h j", h=HEADS),
-                in0=lives_here.to_broadcast([P, HEADS, KERNEL_CHANNELS]),
-                scalar1=1.0 / (LAGS * (N - lag)),
-            )
 
         warm = const.tile([P, 1], F32)
         nc.scalar.activation(out=warm[:], in_=zero_column[:], func=ACT.Exp)
 
+        edges = const.tile([P, 2 * TILES * B * PLANES], F32)
+        edges_nmbt = edges[:].rearrange("q (n m b t) -> q n m b t", n=EDGE_TOKENS, b=B, t=PLANES)
+        edge_words = edge_rows[:].bitcast(F32)
+        edge_bank = transposed.tile([P, BANK], F32, tag="words")
+        for n in range(EDGE_TOKENS):
+            for u in range(HALVES):
+                row = n * ROW_WORDS
+                nc.tensor.transpose(
+                    edge_bank[:, (HALVES * n + u) * P : (HALVES * n + u + 1) * P],
+                    edge_words[:, row + u : row + ROW_WORDS : HALVES],
+                    identity[:],
+                )
+
+        def copy_edges(n):
+            edge_values = edge_bank[:].bitcast(BF16).rearrange(
+                "q (n u x e) -> q n x u e", n=EDGE_TOKENS, u=HALVES, e=WORD
+            )
+            nc.vector.tensor_copy(
+                out=edges[:].rearrange("q (n x u e) -> q n x u e", n=EDGE_TOKENS, u=HALVES, e=WORD)[:, n],
+                in_=edge_values[:, n, 0 : P // 2],
+            )
+
+        def token(k):
+            return edges_nmbt[:, k % EDGE_TOKENS, k // EDGE_TOKENS, :, 0:KERNEL_CHANNELS]
+
+        heads = const.tile([P, LAGS * B * KERNEL_CHANNELS], F32)
+        heads_of_lag = heads[:].rearrange("q (l b j) -> q l b j", l=LAGS, b=B)
+
+        small = products.tile([P, BANK], F32, tag="product")
+        nc.tensor.matmul(
+            out=small[:, 0 : INTER_W + STREAMS], lhsT=ones[:], rhs=vector_rows[:, D:], start=True, stop=True
+        )
+        kernels = small[:, 0:KERNELS]
+        logits = small[:, INTER_W : INTER_W + STREAMS]
+        lives_here = identity[:].rearrange("p (h x) -> p x h", x=HEAD_PARTITIONS)[:, 0:1, :]
         own = weights[:, 2 * SUMS :]
-        nc.vector.tensor_tensor(
-            out=own.rearrange("p (l h j) -> p l h j", l=LAGS, h=HEADS)[:, :, :, 0:LAGS],
-            in0=kernels[:].rearrange("p (h l j) -> p l h j", h=HEADS, l=LAGS),
-            in1=norm[:].rearrange("p (l h j) -> p l h j", l=LAGS, h=HEADS)[:, :, :, 0:LAGS],
-            op=ALU.mult,
-        )
-        top = const.tile([P, 1], F32)
-        nc.vector.tensor_tensor(out=top[:], in0=logits[:, 0:1], in1=logits[:, 1:2], op=ALU.max)
-        minus_top = const.tile([P, 1], F32)
-        nc.vector.tensor_scalar_mul(out=minus_top[:], in0=top[:], scalar1=-1.0)
-        exps = const.tile([P, STREAMS], F32)
-        exp_sum = const.tile([P, 1], F32)
-        nc.scalar.activation(
-            out=exps[:], in_=logits[:], func=ACT.Exp, bias=minus_top[:, 0:1], scale=1.0, accum_out=exp_sum[:, 0:1]
-        )
-        for lag in range(2, LAGS + 1):
+
+        def own_weight(lag):
+            nc.vector.scalar_tensor_tensor(
+                out=own[:, (lag - 1) * SUMS : lag * SUMS].rearrange("p (j h) -> p j h", h=HEADS),
+                in0=kernels.rearrange("p (h l j) -> p l j h", h=HEADS, l=LAGS)[:, lag - 1],
+                scalar=1.0 / (LAGS * (N - lag)),
+                in1=lives_here.to_broadcast([P, KERNEL_CHANNELS, HEADS]),
+                op0=ALU.mult,
+                op1=ALU.mult,
+            )
+
+        def add_weight(lag):
             block = LAGS - lag
             nc.vector.tensor_tensor(
                 out=weights[:, block * SUMS : (block + 1) * SUMS],
@@ -189,70 +215,75 @@ def tile_fieldinteractionoperators_pa_t_kernel(
                 in1=weights[:, (lag + 1) * SUMS : (lag + 2) * SUMS],
                 op=ALU.add,
             )
-        plane_weight = const.tile([P, LAGS * PLANES], F32)
-        nc.vector.tensor_reduce(
-            out=plane_weight[:].rearrange("p (l t) -> p l t", t=PLANES),
-            in_=own.rearrange("p (l h t) -> p l t h", l=LAGS, h=HEADS),
-            axis=AXIS.X,
-            op=ALU.add,
+
+        top = const.tile([P, 1], F32)
+        nc.vector.tensor_reduce(out=top[:], in_=logits, axis=AXIS.X, op=ALU.max)
+        copy_edges(0)
+        minus_top = const.tile([P, 1], F32)
+        nc.vector.tensor_scalar_mul(out=minus_top[:], in0=top[:], scalar1=-1.0)
+        exps = const.tile([P, STREAMS], F32)
+        exp_sum = const.tile([P, 1], F32)
+        nc.scalar.activation(
+            out=exps[:], in_=logits, func=ACT.Exp, bias=minus_top[:, 0:1], scale=1.0, accum_out=exp_sum[:, 0:1]
         )
-
-        heads = const.tile([P, B * LAGS * PLANES], F32)
-        last_tokens = const.tile([P, B * FIELD_SCALES], F32)
-        edge_words = edge_rows[:].bitcast(F32)
-        for u in range(HALVES):
-            edge_bank = transposed.tile([P, BANK], F32, tag="words")
-            for n in range(TILES):
-                row = n * ROW_WORDS
-                nc.tensor.transpose(
-                    edge_bank[:, n * P : (n + 1) * P], edge_words[:, row + u : row + ROW_WORDS : HALVES], identity[:]
-                )
-            edge_values = edge_bank[:].bitcast(BF16).rearrange("q (n c e) -> q n c e", n=TILES, e=WORD)
-            nc.vector.tensor_copy(
-                out=heads[:].rearrange("q (b n u e) -> q n b u e", b=B, u=HALVES, e=WORD)[:, :, :, u, :],
-                in_=edge_values[:, 0:LAGS, 0:B, :],
-            )
-            nc.vector.tensor_copy(
-                out=last_tokens[:].rearrange("q (b n u e) -> q n b u e", b=B, n=TILES, e=WORD)[:, :, :, u, :],
-                in_=edge_values[:, :, B : 2 * B, :],
-            )
-        heads_bnt = heads[:].rearrange("q (b n t) -> q b n t", b=B, t=PLANES)
-        for n in range(1, LAGS):
-            nc.vector.tensor_tensor(
-                out=heads_bnt[:, :, n, :], in0=heads_bnt[:, :, n, :], in1=heads_bnt[:, :, n - 1, :], op=ALU.add
-            )
-
+        copy_edges(1)
+        own_weight(1)
+        own_weight(2)
+        nc.vector.tensor_copy(out=heads_of_lag[:, 0], in_=token(0))
+        own_weight(3)
+        nc.vector.tensor_tensor(out=heads_of_lag[:, 1], in0=token(0), in1=token(1), op=ALU.add)
+        plane_weight = const.tile([P, LAGS * KERNEL_CHANNELS], F32)
+        add_weight(2)
+        nc.vector.tensor_reduce(
+            out=plane_weight[:], in_=own.rearrange("p (x h) -> p x h", h=HEADS), axis=AXIS.X, op=ALU.add
+        )
         inv_sum = const.tile([P, 1], F32)
         nc.vector.reciprocal(out=inv_sum[:], in_=exp_sum[:])
+        nc.vector.tensor_tensor(out=heads_of_lag[:, 2], in0=heads_of_lag[:, 1], in1=token(2), op=ALU.add)
+        add_weight(3)
         iw = const.tile([P, STREAMS], F32)
         nc.vector.tensor_scalar_mul(out=iw[:], in0=exps[:], scalar1=inv_sum[:, 0:1])
+        head_terms = const.tile([P, LAGS * B * KERNEL_CHANNELS], F32)
+        head_terms_of_lag = head_terms[:].rearrange("q (l b j) -> q l b j", l=LAGS, b=B)
+        nc.vector.tensor_tensor(
+            out=head_terms_of_lag,
+            in0=heads_of_lag,
+            in1=plane_weight[:]
+            .rearrange("q (l j) -> q l j", l=LAGS)
+            .unsqueeze(2)
+            .to_broadcast([P, LAGS, B, KERNEL_CHANNELS]),
+            op=ALU.mult,
+        )
         minus_iw0 = const.tile([P, 1], F32)
         nc.vector.tensor_scalar_mul(out=minus_iw0[:], in0=iw[:, 0:1], scalar1=-1.0)
-        total_weight = const.tile([P, (TILES - 1) * SUMS], F32)
-        nc.vector.tensor_scalar_mul(out=total_weight[:], in0=weights[:, 0 : (TILES - 1) * SUMS], scalar1=iw[:, 0:1])
-        head_weight = const.tile([P, LAGS * PLANES], F32)
-        nc.vector.tensor_scalar_mul(out=head_weight[:], in0=plane_weight[:], scalar1=minus_iw0[:, 0:1])
-        nc.vector.memset(terms_all[:].rearrange("q (a m t) -> q a m t", m=SLOTS, t=PLANES)[:, :, SLOTS - 1, :], 1.0)
-        for i in range(TILES - 1):
-            counted = PLANES * (LAGS - i)
-            nc.vector.tensor_tensor(
-                out=terms_all[:].rearrange("q (b i x) -> q b i x", b=B, i=TILES - 1)[:, :, i, SUMS : SUMS + counted],
-                in0=heads[:].rearrange("q (b x) -> q b x", b=B)[:, :, 0:counted],
-                in1=head_weight[:, 0:counted].unsqueeze(1).to_broadcast([P, B, counted]),
-                op=ALU.mult,
-            )
+        total_weight = const.tile([P, SCALED_TILES * SUMS], F32)
+        nc.vector.tensor_scalar_mul(out=total_weight[:], in0=weights[:, 0 : SCALED_TILES * SUMS], scalar1=iw[:, 0:1])
+        bases = terms_all[:].rearrange("q (b i j s) -> q i b j s", b=B, i=SCALED_TILES, s=SLOTS)[:, :, :, :, BASE]
+
+        def base(lag):
+            i = LAGS - lag
+            if lag == 1:
+                nc.vector.tensor_scalar(
+                    out=bases[:, i],
+                    in0=head_terms_of_lag[:, 0],
+                    scalar1=minus_iw0[:, 0:1],
+                    scalar2=1.0,
+                    op0=ALU.mult,
+                    op1=ALU.add,
+                )
+            else:
+                nc.vector.scalar_tensor_tensor(
+                    out=bases[:, i],
+                    in0=head_terms_of_lag[:, lag - 1],
+                    scalar=minus_iw0[:, 0:1],
+                    in1=bases[:, i + 1],
+                    op0=ALU.mult,
+                    op1=ALU.add,
+                )
 
         nl_bias = const.tile([P, PLANES], F32)
-        nc.vector.tensor_scalar_mul(out=nl_bias[:], in0=b3_planes[:], scalar1=iw[:, 1:2])
-
         w3_codes = const.tile([P, D], U32, align_bytes=64)
         w3_scales = const.tile([P, D], U8, align_bytes=64)
-        quantise(weight_to_words(w3_rows), w3_codes, w3_scales)
-
-        out_bias_ps = products.tile([P, BANK], F32, tag="product")
-        nc.tensor.matmul(out=out_bias_ps[:], lhsT=ones[:], rhs=out_b_rows[:], start=True, stop=True)
-        out_bias = const.tile([P, D], F32)
-        nc.vector.tensor_copy(out=out_bias[:], in_=out_bias_ps[:])
 
         h_grouped = {}
         h_codes = {}
@@ -269,31 +300,37 @@ def tile_fieldinteractionoperators_pa_t_kernel(
 
         def total_fields(b):
             total = totals.tile([P, SUMS], F32, tag="total")
-            kernel_channels = f_rows[b][:].rearrange("p (i h x) -> p i h x", i=TILES, h=HEADS)
+            kernel_channels = f_rows[b][:].rearrange("p (i h x) -> p i x h", i=TILES, h=HEADS)[:, :, 0:KERNEL_CHANNELS, :]
             for i in range(TILES):
                 nc.tensor.matmul(
-                    out=total[:].rearrange("p (h j) -> p h j", h=HEADS),
+                    out=total[:].rearrange("p (j h) -> p j h", h=HEADS),
                     lhsT=ones[:],
-                    rhs=kernel_channels[:, i, :, 0:KERNEL_CHANNELS],
+                    rhs=kernel_channels[:, i],
                     start=(i == 0),
                     stop=(i == TILES - 1),
                 )
             field_totals[b] = total
 
+        def entry_terms(b):
+            return terms_all[:, b * TERMS : (b + 1) * TERMS]
+
         def field_scales_products(b):
             nc.vector.tensor_tensor(
-                out=terms_all[:, b * TERMS : (b + 1) * TERMS].rearrange("q (i x) -> q i x", i=TILES - 1)[:, :, 0:SUMS],
-                in0=field_totals[b][:].unsqueeze(1).to_broadcast([P, TILES - 1, SUMS]),
-                in1=total_weight[:].rearrange("q (i x) -> q i x", i=TILES - 1),
+                out=entry_terms(b).rearrange("q (i c s) -> q i c s", i=SCALED_TILES, s=SLOTS)[:, :, :, 0:HEADS],
+                in0=field_totals[b][:]
+                .rearrange("q (c h) -> q c h", h=HEADS)
+                .unsqueeze(1)
+                .to_broadcast([P, SCALED_TILES, KERNEL_CHANNELS, HEADS]),
+                in1=total_weight[:].rearrange("q (i c h) -> q i c h", i=SCALED_TILES, h=HEADS),
                 op=ALU.mult,
             )
 
         def field_scales_sums(b):
             nc.vector.tensor_reduce(
-                out=scales_all[:, b * FIELD_SCALES : b * FIELD_SCALES + (TILES - 1) * PLANES].rearrange(
-                    "q (i t) -> q i t", t=PLANES
-                ),
-                in_=terms_all[:, b * TERMS : (b + 1) * TERMS].rearrange("q (i m t) -> q i t m", m=SLOTS, t=PLANES),
+                out=scales_all[:, b * FIELD_SCALES : (b + 1) * FIELD_SCALES].rearrange("q (i t) -> q i t", t=PLANES)[
+                    :, 0:SCALED_TILES, 0:KERNEL_CHANNELS
+                ],
+                in_=entry_terms(b).rearrange("q (i c s) -> q i c s", i=SCALED_TILES, s=SLOTS),
                 axis=AXIS.X,
                 op=ALU.add,
             )
@@ -301,9 +338,11 @@ def tile_fieldinteractionoperators_pa_t_kernel(
         def scale_last_rows(b):
             scaled = work.tile([P, FIELD_SCALES], F32, tag="last_scaled")
             nc.gpsimd.tensor_tensor(
-                out=scaled[:],
-                in0=last_tokens[:, b * FIELD_SCALES : (b + 1) * FIELD_SCALES],
-                in1=scales_all[:, b * FIELD_SCALES : (b + 1) * FIELD_SCALES],
+                out=scaled[:].rearrange("q (m n t) -> q m n t", n=EDGE_TOKENS, t=PLANES),
+                in0=edges_nmbt[:, :, TILES // EDGE_TOKENS :, b, :].rearrange("q n m t -> q m n t"),
+                in1=scales_all[:, b * FIELD_SCALES : (b + 1) * FIELD_SCALES].rearrange(
+                    "q (m n t) -> q m n t", n=EDGE_TOKENS, t=PLANES
+                ),
                 op=ALU.mult,
             )
             last_scaled[b] = scaled
@@ -320,7 +359,8 @@ def tile_fieldinteractionoperators_pa_t_kernel(
             if pair == 0:
                 grouped = work.tile([P, PLANES * N], BF16, tag="h_grouped", align_bytes=64)
                 h_grouped[b] = grouped
-            rows_to_words(h_rows[b], h_grouped[b], pair)
+            bank = transposed.tile([P, BANK], F32, tag="words")
+            rows_to_words(h_rows[b], h_grouped[b], pair, bank, nc.scalar.copy)
 
         def transpose_fields(b, u):
             if u == 0:
@@ -384,7 +424,7 @@ def tile_fieldinteractionoperators_pa_t_kernel(
             e_codes[b] = codes
             e_scales[b] = scales
 
-        def second_product_and_store(b, i, on_scalar):
+        def second_product(b, i, on_scalar):
             if i == 0:
                 result = rows_out.tile([P, TILES * D], F32, tag="result")
                 results[b] = result
@@ -407,52 +447,79 @@ def tile_fieldinteractionoperators_pa_t_kernel(
                 )
             else:
                 nc.vector.tensor_tensor(out=results[b][:, columns], in0=projected[:], in1=out_bias[:], op=ALU.add)
-            if i % 2 == 1:
-                half = slice((i - 1) * D, (i + 1) * D)
-                nc.sync.dma_start(out=out[b].rearrange("(p i) o -> p (i o)", i=TILES)[:, half], in_=results[b][:, half])
+
+        def store(b, first, tiles):
+            run = slice(first * D, (first + tiles) * D)
+            nc.sync.dma_start(out=out[b].rearrange("(p i) o -> p (i o)", i=TILES)[:, run], in_=results[b][:, run])
 
         def entry(b):
             return 0 <= b < B
 
-        def transpose_a_bank(j, k):
-            if k < TILES // BLOCKS_IN_BANK:
-                if entry(j + H_AHEAD):
-                    transpose_h(j + H_AHEAD, k)
-            elif entry(j + FIELDS_AHEAD):
-                transpose_fields(j + FIELDS_AHEAD, k - TILES // BLOCKS_IN_BANK)
-
         def step(j):
-            if PRELOADED <= j + LOADS_AHEAD < B:
-                load(j + LOADS_AHEAD)
+            if entry(j + LOADS_AHEAD):
+                load_h(j + LOADS_AHEAD)
+                load_fields(j + LOADS_AHEAD)
             if entry(j + FIELDS_AHEAD):
                 field_scales_products(j + FIELDS_AHEAD)
                 quantise_h(j + FIELDS_AHEAD)
                 field_scales_sums(j + FIELDS_AHEAD)
                 scale_last_rows(j + FIELDS_AHEAD)
-            tiles_on_scalar = OUT_TILES_ON_SCALAR if entry(j) else 0
-            if entry(j - SECOND_PRODUCT_BEHIND):
-                for i in range(tiles_on_scalar):
-                    second_product_and_store(j - SECOND_PRODUCT_BEHIND, i, True)
-            for i in range(TILES):
+            done = j - SECOND_PRODUCT_BEHIND
+            last = done == B - 1
+            tiles_on_scalar = LAST_OUT_TILES_ON_SCALAR if last else OUT_TILES_ON_SCALAR
+            for half in (range(TILES // 2), range(TILES // 2, TILES)):
+                first_half = half.start == 0
                 if entry(j):
-                    first_product_and_fusion(j, i)
-                if (i + 1) % BANKS_IN_RUN == 0:
-                    for k in range(i + 1 - BANKS_IN_RUN, i + 1):
-                        transpose_a_bank(j, k)
+                    for i in half:
+                        first_product_and_fusion(j, i)
+                        if entry(done) and not first_half:
+                            second_product(done, i, False)
+                if entry(done) and (first_half or not entry(j)):
+                    for i in half:
+                        second_product(done, i, i < tiles_on_scalar)
+                if entry(done) and not last:
+                    store(done, half.start, len(half))
+                if first_half and entry(j + FIELDS_AHEAD):
+                    for u in range(HALVES):
+                        transpose_fields(j + FIELDS_AHEAD, u)
+                if not first_half and entry(j + H_AHEAD):
+                    for pair in range(TILES // BLOCKS_IN_BANK):
+                        transpose_h(j + H_AHEAD, pair)
             if entry(j + FIELDS_AHEAD):
                 write_last_rows(j + FIELDS_AHEAD)
-            if entry(j - SECOND_PRODUCT_BEHIND):
-                for i in range(tiles_on_scalar, TILES):
-                    second_product_and_store(j - SECOND_PRODUCT_BEHIND, i, False)
             if entry(j):
                 quantise_enhanced(j)
             if entry(j + H_AHEAD):
                 total_fields(j + H_AHEAD)
+            if last:
+                for i in [*range(tiles_on_scalar, TILES), *range(tiles_on_scalar)]:
+                    store(done, i, 1)
 
-        for j in range(FIRST_STEP, SECOND_PRODUCT_BEHIND - 1):
-            step(j)
+        for k in range(TILES // BLOCKS_IN_BANK):
+            transpose_h(0, k)
+        total_fields(0)
+        base(1)
+        field_scales_products(0)
+        base(2)
+        nc.vector.tensor_scalar_mul(out=nl_bias[:], in0=b3_planes[:], scalar1=iw[:, 1:2])
+        base(3)
+        w3_grouped = weight_to_words(w3_rows)
+        field_scales_sums(0)
+        scale_last_rows(0)
+        for k in range(TILES // BLOCKS_IN_BANK):
+            transpose_h(1, k)
+        quantise_h(0)
+        for u in range(HALVES):
+            transpose_fields(0, u)
+        quantise(w3_grouped, w3_codes, w3_scales)
+        write_last_rows(0)
+        total_fields(1)
         out_w_grouped = weight_to_words(out_w_rows)
-        step(SECOND_PRODUCT_BEHIND - 1)
+        step(0)
         quantise(out_w_grouped, out_w_codes, out_w_scales)
+        out_bias_ps = products.tile([P, BANK], F32, tag="product")
+        nc.tensor.matmul(out=out_bias_ps[:], lhsT=ones[:], rhs=vector_rows[:, 0:D], start=True, stop=True)
+        out_bias = const.tile([P, D], F32)
+        nc.vector.tensor_copy(out=out_bias[:], in_=out_bias_ps[:])
         for j in range(SECOND_PRODUCT_BEHIND, B + SECOND_PRODUCT_BEHIND):
             step(j)

@@ -41,16 +41,17 @@ TERMS = SCALED_TILES * KERNEL_CHANNELS * SLOTS
 FIELD_SCALES = TILES * PLANES
 
 LOADS_AHEAD = 6
-H_AHEAD = 2
+H_AHEAD = 3
+PREPARED_AHEAD = 2
 FIELDS_AHEAD = 1
 SECOND_PRODUCT_BEHIND = 1
 OUT_TILES_ON_SCALAR = 2
+EARLY_TILES = 3
 LAST_OUT_TILES_ON_SCALAR = 1
 WORK_BUFFERS = 2
 RESULT_BUFFERS = 3
 WORD_BANKS = 3
-PRODUCT_BANKS = 4
-TOTAL_BANKS = 1
+PRODUCT_BANKS = 5
 
 FLOPS = 2 * 2 * B * N * D * D
 
@@ -67,7 +68,6 @@ def tile_fieldinteractionoperators_pa_t_kernel(
         rows_out = ctx.enter_context(tc.tile_pool(name="rows_out", bufs=RESULT_BUFFERS))
         transposed = ctx.enter_context(tc.psum_pool(name="transposed", bufs=WORD_BANKS))
         products = ctx.enter_context(tc.psum_pool(name="products", bufs=PRODUCT_BANKS))
-        totals = ctx.enter_context(tc.psum_pool(name="totals", bufs=TOTAL_BANKS))
 
         identity = const.tile([P, P], F32)
         make_identity(nc, identity[:])
@@ -299,11 +299,12 @@ def tile_fieldinteractionoperators_pa_t_kernel(
         out_w_scales = const.tile([P, D], U8, align_bytes=64)
 
         def total_fields(b):
-            total = totals.tile([P, SUMS], F32, tag="total")
+            bank = products.tile([P, BANK], F32, tag="product")
+            total = bank[:, 0:SUMS]
             kernel_channels = f_rows[b][:].rearrange("p (i h x) -> p i x h", i=TILES, h=HEADS)[:, :, 0:KERNEL_CHANNELS, :]
             for i in range(TILES):
                 nc.tensor.matmul(
-                    out=total[:].rearrange("p (j h) -> p j h", h=HEADS),
+                    out=total.rearrange("p (j h) -> p j h", h=HEADS),
                     lhsT=ones[:],
                     rhs=kernel_channels[:, i],
                     start=(i == 0),
@@ -317,7 +318,7 @@ def tile_fieldinteractionoperators_pa_t_kernel(
         def field_scales_products(b):
             nc.vector.tensor_tensor(
                 out=entry_terms(b).rearrange("q (i c s) -> q i c s", i=SCALED_TILES, s=SLOTS)[:, :, :, 0:HEADS],
-                in0=field_totals[b][:]
+                in0=field_totals[b]
                 .rearrange("q (c h) -> q c h", h=HEADS)
                 .unsqueeze(1)
                 .to_broadcast([P, SCALED_TILES, KERNEL_CHANNELS, HEADS]),
@@ -417,12 +418,17 @@ def tile_fieldinteractionoperators_pa_t_kernel(
                 op1=ALU.add,
             )
 
-        def quantise_enhanced(b):
-            codes = work.tile([P, N], U32, tag="e_codes", align_bytes=64)
-            scales = work.tile([P, N], U8, tag="e_scales", align_bytes=64)
-            quantise(enhanced[b], codes, scales)
-            e_codes[b] = codes
-            e_scales[b] = scales
+        def quantise_enhanced(b, tokens):
+            if tokens.start == 0:
+                codes = work.tile([P, N], U32, tag="e_codes", align_bytes=64)
+                scales = work.tile([P, N], U8, tag="e_scales", align_bytes=64)
+                e_codes[b] = codes
+                e_scales[b] = scales
+            nc.vector.quantize_mx(
+                out=e_codes[b][:, tokens].bitcast(FP8X4),
+                scales=e_scales[b][:, tokens],
+                in_=enhanced[b][:, PLANES * tokens.start : PLANES * tokens.stop],
+            )
 
         def second_product(b, i, on_scalar):
             if i == 0:
@@ -459,44 +465,58 @@ def tile_fieldinteractionoperators_pa_t_kernel(
             if entry(j + LOADS_AHEAD):
                 load_h(j + LOADS_AHEAD)
                 load_fields(j + LOADS_AHEAD)
-            if entry(j + FIELDS_AHEAD):
-                field_scales_products(j + FIELDS_AHEAD)
-                quantise_h(j + FIELDS_AHEAD)
-                field_scales_sums(j + FIELDS_AHEAD)
-                scale_last_rows(j + FIELDS_AHEAD)
             done = j - SECOND_PRODUCT_BEHIND
             last = done == B - 1
             tiles_on_scalar = LAST_OUT_TILES_ON_SCALAR if last else OUT_TILES_ON_SCALAR
-            for half in (range(TILES // 2), range(TILES // 2, TILES)):
-                first_half = half.start == 0
-                if entry(j):
-                    for i in half:
-                        first_product_and_fusion(j, i)
-                        if entry(done) and not first_half:
-                            second_product(done, i, False)
-                if entry(done) and (first_half or not entry(j)):
-                    for i in half:
-                        second_product(done, i, i < tiles_on_scalar)
-                if entry(done) and not last:
-                    store(done, half.start, len(half))
-                if first_half and entry(j + FIELDS_AHEAD):
-                    for u in range(HALVES):
-                        transpose_fields(j + FIELDS_AHEAD, u)
-                if not first_half and entry(j + H_AHEAD):
+            on_scalar = range(tiles_on_scalar) if entry(done) else ()
+            on_vector = range(tiles_on_scalar, TILES) if entry(done) else ()
+            if entry(j):
+                for i in range(EARLY_TILES):
+                    first_product_and_fusion(j, i)
+            for i in on_scalar:
+                second_product(done, i, True)
+            if entry(done) and not last:
+                store(done, 0, tiles_on_scalar)
+            if j == B - 1:
+                quantise_enhanced(j, slice(0, N // 2))
+            if entry(j + FIELDS_AHEAD):
+                for u in range(HALVES):
+                    transpose_fields(j + FIELDS_AHEAD, u)
+            for i in on_vector:
+                second_product(done, i, False)
+                if entry(j) and i == on_vector[0]:
+                    first_product_and_fusion(j, EARLY_TILES)
+            if entry(done) and not last:
+                store(done, tiles_on_scalar, TILES - tiles_on_scalar)
+            if j == 0:
+                first_product_and_fusion(j, EARLY_TILES)
+            if entry(j + PREPARED_AHEAD):
+                total_fields(j + PREPARED_AHEAD)
+            for b in range(H_AHEAD - 1 if j == 0 else j + H_AHEAD, j + H_AHEAD + 1):
+                if entry(b):
                     for pair in range(TILES // BLOCKS_IN_BANK):
-                        transpose_h(j + H_AHEAD, pair)
+                        transpose_h(b, pair)
             if entry(j + FIELDS_AHEAD):
                 write_last_rows(j + FIELDS_AHEAD)
-            if entry(j):
-                quantise_enhanced(j)
-            if entry(j + H_AHEAD):
-                total_fields(j + H_AHEAD)
+            if entry(j + PREPARED_AHEAD):
+                field_scales_products(j + PREPARED_AHEAD)
+            if j == B - 1:
+                quantise_enhanced(j, slice(N // 2, N))
+            elif entry(j):
+                quantise_enhanced(j, slice(0, N))
+            if entry(j + PREPARED_AHEAD):
+                quantise_h(j + PREPARED_AHEAD)
+                field_scales_sums(j + PREPARED_AHEAD)
+                scale_last_rows(j + PREPARED_AHEAD)
             if last:
                 for i in [*range(tiles_on_scalar, TILES), *range(tiles_on_scalar)]:
                     store(done, i, 1)
 
-        for k in range(TILES // BLOCKS_IN_BANK):
-            transpose_h(0, k)
+        def transpose_entry_h(b):
+            for pair in range(TILES // BLOCKS_IN_BANK):
+                transpose_h(b, pair)
+
+        transpose_entry_h(0)
         total_fields(0)
         base(1)
         field_scales_products(0)
@@ -506,20 +526,22 @@ def tile_fieldinteractionoperators_pa_t_kernel(
         w3_grouped = weight_to_words(w3_rows)
         field_scales_sums(0)
         scale_last_rows(0)
-        for k in range(TILES // BLOCKS_IN_BANK):
-            transpose_h(1, k)
+        transpose_entry_h(1)
         quantise_h(0)
         for u in range(HALVES):
             transpose_fields(0, u)
         quantise(w3_grouped, w3_codes, w3_scales)
         write_last_rows(0)
         total_fields(1)
-        out_w_grouped = weight_to_words(out_w_rows)
+        field_scales_products(1)
+        quantise_h(1)
+        field_scales_sums(1)
+        scale_last_rows(1)
+        quantise(weight_to_words(out_w_rows), out_w_codes, out_w_scales)
         step(0)
-        quantise(out_w_grouped, out_w_codes, out_w_scales)
         out_bias_ps = products.tile([P, BANK], F32, tag="product")
         nc.tensor.matmul(out=out_bias_ps[:], lhsT=ones[:], rhs=vector_rows[:, 0:D], start=True, stop=True)
         out_bias = const.tile([P, D], F32)
-        nc.vector.tensor_copy(out=out_bias[:], in_=out_bias_ps[:])
+        nc.scalar.copy(out=out_bias[:], in_=out_bias_ps[:])
         for j in range(SECOND_PRODUCT_BEHIND, B + SECOND_PRODUCT_BEHIND):
             step(j)

@@ -45,9 +45,9 @@ H_AHEAD = 3
 PREPARED_AHEAD = 2
 FIELDS_AHEAD = 1
 SECOND_PRODUCT_BEHIND = 1
-OUT_TILES_ON_SCALAR = 2
-EARLY_TILES = 3
-LAST_OUT_TILES_ON_SCALAR = 1
+TILES_ON_GPSIMD = (0, 1)
+EARLY_TILE_ON_VECTOR = 2
+LATE_TILE_ON_VECTOR = 3
 WORK_BUFFERS = 2
 RESULT_BUFFERS = 3
 WORD_BANKS = 3
@@ -393,7 +393,7 @@ def tile_fieldinteractionoperators_pa_t_kernel(
             h_scales[b] = scales
 
         def first_product_and_fusion(b, i):
-            if i == 0:
+            if i == TILES_ON_GPSIMD[0]:
                 fused = work.tile([P, PLANES * N], BF16, tag="enhanced", align_bytes=64)
                 enhanced[b] = fused
             tokens = slice(i * P, (i + 1) * P)
@@ -409,17 +409,21 @@ def tile_fieldinteractionoperators_pa_t_kernel(
                     start=True,
                     stop=True,
                 )
-            nc.vector.scalar_tensor_tensor(
-                out=enhanced[b][:, i * BANK : (i + 1) * BANK].rearrange("q (r t) -> q r t", t=PLANES),
-                in0=nl[:].rearrange("q (t r) -> q r t", t=PLANES),
-                scalar=iw[:, 1:2],
-                in1=field_terms[b][:].rearrange("q (t i r) -> q i r t", t=PLANES, i=TILES)[:, i],
-                op0=ALU.mult,
-                op1=ALU.add,
-            )
+            alternately = nl[:].rearrange("q (t r) -> q r t", t=PLANES)
+            fused_tile = enhanced[b][:, i * BANK : (i + 1) * BANK].rearrange("q (r t) -> q r t", t=PLANES)
+            field_term = field_terms[b][:].rearrange("q (t i r) -> q i r t", t=PLANES, i=TILES)[:, i]
+            if i in TILES_ON_GPSIMD:
+                weighted = work.tile([P, BANK], F32, tag="weighted")
+                weighted_tile = weighted[:].rearrange("q (r t) -> q r t", t=PLANES)
+                nc.scalar.activation(out=weighted_tile, in_=alternately, func=ACT.Copy, scale=iw[:, 1:2])
+                nc.gpsimd.tensor_tensor(out=fused_tile, in0=weighted_tile, in1=field_term, op=ALU.add)
+            else:
+                nc.vector.scalar_tensor_tensor(
+                    out=fused_tile, in0=alternately, scalar=iw[:, 1:2], in1=field_term, op0=ALU.mult, op1=ALU.add
+                )
 
         def quantise_enhanced(b, tokens):
-            if tokens.start == 0:
+            if b not in e_codes:
                 codes = work.tile([P, N], U32, tag="e_codes", align_bytes=64)
                 scales = work.tile([P, N], U8, tag="e_scales", align_bytes=64)
                 e_codes[b] = codes
@@ -430,8 +434,8 @@ def tile_fieldinteractionoperators_pa_t_kernel(
                 in_=enhanced[b][:, PLANES * tokens.start : PLANES * tokens.stop],
             )
 
-        def second_product(b, i, on_scalar):
-            if i == 0:
+        def second_product(b, i):
+            if b not in results:
                 result = rows_out.tile([P, TILES * D], F32, tag="result")
                 results[b] = result
             tokens = slice(i * P, (i + 1) * P)
@@ -446,13 +450,7 @@ def tile_fieldinteractionoperators_pa_t_kernel(
                 start=True,
                 stop=True,
             )
-            if on_scalar:
-                nc.scalar.copy(out=results[b][:, columns], in_=projected[:])
-                nc.gpsimd.tensor_tensor(
-                    out=results[b][:, columns], in0=results[b][:, columns], in1=out_bias[:], op=ALU.add
-                )
-            else:
-                nc.vector.tensor_tensor(out=results[b][:, columns], in0=projected[:], in1=out_bias[:], op=ALU.add)
+            nc.vector.tensor_tensor(out=results[b][:, columns], in0=projected[:], in1=out_bias[:], op=ALU.add)
 
         def store(b, first, tiles):
             run = slice(first * D, (first + tiles) * D)
@@ -466,51 +464,40 @@ def tile_fieldinteractionoperators_pa_t_kernel(
                 load_h(j + LOADS_AHEAD)
                 load_fields(j + LOADS_AHEAD)
             done = j - SECOND_PRODUCT_BEHIND
-            last = done == B - 1
-            tiles_on_scalar = LAST_OUT_TILES_ON_SCALAR if last else OUT_TILES_ON_SCALAR
-            on_scalar = range(tiles_on_scalar) if entry(done) else ()
-            on_vector = range(tiles_on_scalar, TILES) if entry(done) else ()
-            if entry(j):
-                for i in range(EARLY_TILES):
-                    first_product_and_fusion(j, i)
-            for i in on_scalar:
-                second_product(done, i, True)
-            if entry(done) and not last:
-                store(done, 0, tiles_on_scalar)
-            if j == B - 1:
-                quantise_enhanced(j, slice(0, N // 2))
+            last = j == B - 1
+            for i in TILES_ON_GPSIMD:
+                first_product_and_fusion(j, i)
+            first_product_and_fusion(j, EARLY_TILE_ON_VECTOR)
+            if last:
+                first_product_and_fusion(j, LATE_TILE_ON_VECTOR)
+                quantise_enhanced(j, slice(N // 2, N))
+            if entry(done):
+                for i in range(TILES // 2):
+                    second_product(done, i)
+                store(done, 0, TILES // 2)
             if entry(j + FIELDS_AHEAD):
                 for u in range(HALVES):
                     transpose_fields(j + FIELDS_AHEAD, u)
-            for i in on_vector:
-                second_product(done, i, False)
-                if entry(j) and i == on_vector[0]:
-                    first_product_and_fusion(j, EARLY_TILES)
-            if entry(done) and not last:
-                store(done, tiles_on_scalar, TILES - tiles_on_scalar)
-            if j == 0:
-                first_product_and_fusion(j, EARLY_TILES)
+                write_last_rows(j + FIELDS_AHEAD)
+            if not last:
+                first_product_and_fusion(j, LATE_TILE_ON_VECTOR)
+            if entry(done):
+                for i in range(TILES // 2, TILES):
+                    second_product(done, i)
+                store(done, TILES // 2, TILES // 2)
             if entry(j + PREPARED_AHEAD):
                 total_fields(j + PREPARED_AHEAD)
             for b in range(H_AHEAD - 1 if j == 0 else j + H_AHEAD, j + H_AHEAD + 1):
                 if entry(b):
                     for pair in range(TILES // BLOCKS_IN_BANK):
                         transpose_h(b, pair)
-            if entry(j + FIELDS_AHEAD):
-                write_last_rows(j + FIELDS_AHEAD)
             if entry(j + PREPARED_AHEAD):
                 field_scales_products(j + PREPARED_AHEAD)
-            if j == B - 1:
-                quantise_enhanced(j, slice(N // 2, N))
-            elif entry(j):
-                quantise_enhanced(j, slice(0, N))
+            quantise_enhanced(j, slice(0, N // 2 if last else N))
             if entry(j + PREPARED_AHEAD):
                 quantise_h(j + PREPARED_AHEAD)
                 field_scales_sums(j + PREPARED_AHEAD)
                 scale_last_rows(j + PREPARED_AHEAD)
-            if last:
-                for i in [*range(tiles_on_scalar, TILES), *range(tiles_on_scalar)]:
-                    store(done, i, 1)
 
         def transpose_entry_h(b):
             for pair in range(TILES // BLOCKS_IN_BANK):
@@ -543,5 +530,8 @@ def tile_fieldinteractionoperators_pa_t_kernel(
         nc.tensor.matmul(out=out_bias_ps[:], lhsT=ones[:], rhs=vector_rows[:, 0:D], start=True, stop=True)
         out_bias = const.tile([P, D], F32)
         nc.scalar.copy(out=out_bias[:], in_=out_bias_ps[:])
-        for j in range(SECOND_PRODUCT_BEHIND, B + SECOND_PRODUCT_BEHIND):
+        for j in range(1, B):
             step(j)
+        for i in [*range(TILES // 2, TILES), *range(TILES // 2)]:
+            second_product(B - 1, i)
+            store(B - 1, i, 1)

@@ -45,9 +45,9 @@ H_AHEAD = 3
 PREPARED_AHEAD = 2
 FIELDS_AHEAD = 1
 SECOND_PRODUCT_BEHIND = 1
-TILES_ON_GPSIMD = (0, 1)
-EARLY_TILE_ON_VECTOR = 2
-LATE_TILE_ON_VECTOR = 3
+FUSION_ON_GPSIMD = 0
+OUT_TILE_ON_GPSIMD = 0
+EARLY_TILES = 3
 WORK_BUFFERS = 2
 RESULT_BUFFERS = 3
 WORD_BANKS = 3
@@ -393,7 +393,7 @@ def tile_fieldinteractionoperators_pa_t_kernel(
             h_scales[b] = scales
 
         def first_product_and_fusion(b, i):
-            if i == TILES_ON_GPSIMD[0]:
+            if i == 0:
                 fused = work.tile([P, PLANES * N], BF16, tag="enhanced", align_bytes=64)
                 enhanced[b] = fused
             tokens = slice(i * P, (i + 1) * P)
@@ -412,7 +412,7 @@ def tile_fieldinteractionoperators_pa_t_kernel(
             alternately = nl[:].rearrange("q (t r) -> q r t", t=PLANES)
             fused_tile = enhanced[b][:, i * BANK : (i + 1) * BANK].rearrange("q (r t) -> q r t", t=PLANES)
             field_term = field_terms[b][:].rearrange("q (t i r) -> q i r t", t=PLANES, i=TILES)[:, i]
-            if i in TILES_ON_GPSIMD:
+            if i == FUSION_ON_GPSIMD:
                 weighted = work.tile([P, BANK], F32, tag="weighted")
                 weighted_tile = weighted[:].rearrange("q (r t) -> q r t", t=PLANES)
                 nc.scalar.activation(out=weighted_tile, in_=alternately, func=ACT.Copy, scale=iw[:, 1:2])
@@ -434,7 +434,7 @@ def tile_fieldinteractionoperators_pa_t_kernel(
                 in_=enhanced[b][:, PLANES * tokens.start : PLANES * tokens.stop],
             )
 
-        def second_product(b, i):
+        def second_product(b, i, on_gpsimd=False):
             if b not in results:
                 result = rows_out.tile([P, TILES * D], F32, tag="result")
                 results[b] = result
@@ -450,7 +450,13 @@ def tile_fieldinteractionoperators_pa_t_kernel(
                 start=True,
                 stop=True,
             )
-            nc.vector.tensor_tensor(out=results[b][:, columns], in0=projected[:], in1=out_bias[:], op=ALU.add)
+            if on_gpsimd:
+                nc.scalar.copy(out=results[b][:, columns], in_=projected[:])
+                nc.gpsimd.tensor_tensor(
+                    out=results[b][:, columns], in0=results[b][:, columns], in1=out_bias[:], op=ALU.add
+                )
+            else:
+                nc.vector.tensor_tensor(out=results[b][:, columns], in0=projected[:], in1=out_bias[:], op=ALU.add)
 
         def store(b, first, tiles):
             run = slice(first * D, (first + tiles) * D)
@@ -465,22 +471,20 @@ def tile_fieldinteractionoperators_pa_t_kernel(
                 load_fields(j + LOADS_AHEAD)
             done = j - SECOND_PRODUCT_BEHIND
             last = j == B - 1
-            for i in TILES_ON_GPSIMD:
+            for i in range(TILES if last else EARLY_TILES):
                 first_product_and_fusion(j, i)
-            first_product_and_fusion(j, EARLY_TILE_ON_VECTOR)
             if last:
-                first_product_and_fusion(j, LATE_TILE_ON_VECTOR)
                 quantise_enhanced(j, slice(N // 2, N))
             if entry(done):
                 for i in range(TILES // 2):
-                    second_product(done, i)
+                    second_product(done, i, i == OUT_TILE_ON_GPSIMD and not last)
                 store(done, 0, TILES // 2)
             if entry(j + FIELDS_AHEAD):
                 for u in range(HALVES):
                     transpose_fields(j + FIELDS_AHEAD, u)
                 write_last_rows(j + FIELDS_AHEAD)
             if not last:
-                first_product_and_fusion(j, LATE_TILE_ON_VECTOR)
+                first_product_and_fusion(j, EARLY_TILES)
             if entry(done):
                 for i in range(TILES // 2, TILES):
                     second_product(done, i)

@@ -49,6 +49,7 @@ FUSION_ON_GPSIMD = 0
 OUT_TILE_ON_GPSIMD = 0
 EARLY_TILES = 3
 WORK_BUFFERS = 2
+H_BUFFERS = 3
 RESULT_BUFFERS = 3
 WORD_BANKS = 3
 PRODUCT_BANKS = 5
@@ -63,7 +64,7 @@ def tile_fieldinteractionoperators_pa_t_kernel(
     with ExitStack() as ctx:
         ctx.enter_context(tc.manual_schedule())
         const = ctx.enter_context(tc.tile_pool(name="const", bufs=1))
-        rows_in = ctx.enter_context(tc.tile_pool(name="rows_in", bufs=LOADS_AHEAD))
+        rows_in = ctx.enter_context(tc.tile_pool(name="rows_in", bufs=LOADS_AHEAD + 1))
         work = ctx.enter_context(tc.tile_pool(name="work", bufs=WORK_BUFFERS))
         rows_out = ctx.enter_context(tc.tile_pool(name="rows_out", bufs=RESULT_BUFFERS))
         transposed = ctx.enter_context(tc.psum_pool(name="transposed", bufs=WORD_BANKS))
@@ -73,16 +74,18 @@ def tile_fieldinteractionoperators_pa_t_kernel(
         make_identity(nc, identity[:])
         terms_all = const.tile([P, B * TERMS], F32)
 
-        zero_column = const.tile([P, 1], F32)
-        nc.vector.memset(zero_column[:], 0.0)
         vector_rows = const.tile([P, D + INTER_W + STREAMS], BF16)
         nc.vector.memset(vector_rows[:], 0.0)
+        zero_column = const.tile([P, 1], F32)
+        nc.vector.memset(zero_column[:], 0.0)
         edge_rows = const.tile([P, EDGE_TOKENS * D], BF16)
         nc.gpsimd.memset(edge_rows[P // 2 :, :], 0.0)
         ones = const.tile([P, P], BF16)
         nc.vector.memset(ones[:], 1.0)
         scales_all = const.tile([P, B * FIELD_SCALES], F32)
         nc.vector.memset(scales_all[:], 1.0)
+        identity_bf16 = const.tile([P, P], BF16)
+        nc.vector.tensor_copy(out=identity_bf16[:], in_=identity[:])
         weights = const.tile([P, (LAGS + 2) * SUMS], F32)
 
         h_rows = {}
@@ -99,10 +102,10 @@ def tile_fieldinteractionoperators_pa_t_kernel(
             f_rows[b] = f_tile
 
         for m in range(2 * TILES // EDGE_TOKENS):
-            token = EDGE_TOKENS * m if m < TILES // EDGE_TOKENS else N - 2 * TILES + EDGE_TOKENS * m
+            first_token = EDGE_TOKENS * m if m < TILES // EDGE_TOKENS else N - 2 * TILES + EDGE_TOKENS * m
             nc.sync.dma_start(
                 out=edge_rows[B * m : B * (m + 1), :],
-                in_=fields[:, token : token + EDGE_TOKENS, :].rearrange("b n c -> b (n c)"),
+                in_=fields[:, first_token : first_token + EDGE_TOKENS, :].rearrange("b n c -> b (n c)"),
             )
         nc.sync.dma_start(
             out=vector_rows[0:1, D + INTER_W : D + INTER_W + STREAMS], in_=inter_w.rearrange("(o s) -> o s", o=1)
@@ -116,15 +119,13 @@ def tile_fieldinteractionoperators_pa_t_kernel(
         nc.sync.dma_start(out=w3_rows[:], in_=w3.rearrange("(m t) k -> m (t k)", t=PLANES))
         b3_planes = const.tile([P, PLANES], BF16)
         nc.sync.dma_start(out=b3_planes[:], in_=b3.rearrange("(q t) -> q t", t=PLANES))
-        load_h(1)
         out_w_rows = const.tile([P, ROW], BF16)
         nc.sync.dma_start(
             out=out_w_rows[:].rearrange("m (a k) -> m a k", a=TILES),
             in_=out_w.rearrange("(a m) k -> m a k", a=TILES),
         )
         nc.sync.dma_start(out=vector_rows[0:1, 0:D], in_=out_b.rearrange("(o c) -> o c", o=1))
-        load_fields(1)
-        for b in range(2, LOADS_AHEAD):
+        for b in range(1, LOADS_AHEAD + 1):
             load_h(b)
             load_fields(b)
 
@@ -149,11 +150,11 @@ def tile_fieldinteractionoperators_pa_t_kernel(
         def quantise(grouped, codes, scales):
             nc.vector.quantize_mx(out=codes[:].bitcast(FP8X4), scales=scales[:], in_=grouped[:])
 
-        def weight_to_words(rows):
+        def weight_to_words(rows, copy):
             grouped = work.tile([P, PLANES * D], BF16, tag="weight_grouped", align_bytes=64)
             for pair in range(TILES // BLOCKS_IN_BANK):
                 bank = products.tile([P, BANK], F32, tag="product")
-                rows_to_words(rows, grouped, pair, bank, nc.vector.tensor_copy)
+                rows_to_words(rows, grouped, pair, bank, copy)
             return grouped
 
 
@@ -173,6 +174,11 @@ def tile_fieldinteractionoperators_pa_t_kernel(
                     identity[:],
                 )
 
+        small = products.tile([P, BANK], F32, tag="product")
+        nc.tensor.matmul(
+            out=small[:, 0 : INTER_W + STREAMS], lhsT=ones[:], rhs=vector_rows[:, D:], start=True, stop=True
+        )
+
         def copy_edges(n):
             edge_values = edge_bank[:].bitcast(BF16).rearrange(
                 "q (n u x e) -> q n x u e", n=EDGE_TOKENS, u=HALVES, e=WORD
@@ -188,10 +194,6 @@ def tile_fieldinteractionoperators_pa_t_kernel(
         heads = const.tile([P, LAGS * B * KERNEL_CHANNELS], F32)
         heads_of_lag = heads[:].rearrange("q (l b j) -> q l b j", l=LAGS, b=B)
 
-        small = products.tile([P, BANK], F32, tag="product")
-        nc.tensor.matmul(
-            out=small[:, 0 : INTER_W + STREAMS], lhsT=ones[:], rhs=vector_rows[:, D:], start=True, stop=True
-        )
         kernels = small[:, 0:KERNELS]
         logits = small[:, INTER_W : INTER_W + STREAMS]
         lives_here = identity[:].rearrange("p (h x) -> p x h", x=HEAD_PARTITIONS)[:, 0:1, :]
@@ -358,32 +360,44 @@ def tile_fieldinteractionoperators_pa_t_kernel(
 
         def transpose_h(b, pair):
             if pair == 0:
-                grouped = work.tile([P, PLANES * N], BF16, tag="h_grouped", align_bytes=64)
+                grouped = work.tile([P, PLANES * N], BF16, tag="h_grouped", bufs=H_BUFFERS, align_bytes=64)
                 h_grouped[b] = grouped
             bank = transposed.tile([P, BANK], F32, tag="words")
             rows_to_words(h_rows[b], h_grouped[b], pair, bank, nc.scalar.copy)
 
-        def transpose_fields(b, u):
-            if u == 0:
-                term = work.tile([P, PLANES * N], F32, tag="field_term")
-                field_terms[b] = term
-            f_words = f_rows[b][:].bitcast(F32)
-            bank = transposed.tile([P, BANK], F32, tag="words")
-            for i in range(TILES):
-                row = i * ROW_WORDS
-                nc.tensor.transpose(
-                    bank[:, i * P : (i + 1) * P], f_words[:, row + u : row + ROW_WORDS : HALVES], identity[:]
-                )
-            values = bank[:].bitcast(BF16).rearrange("q (x e) -> q x e", e=WORD)
-            for e in range(WORD):
-                t = WORD * u + e
+        def transpose_fields(b):
+            term = work.tile([P, PLANES * N], F32, tag="field_term")
+            field_terms[b] = term
+
+            def scale_plane(t, values):
                 nc.scalar.activation(
                     out=field_terms[b][:, t * N : (t + 1) * N],
-                    in_=values[:, :, e],
+                    in_=values,
                     func=ACT.Identity,
                     bias=nl_bias[:, t : t + 1],
                     scale=scales_all[:, b * FIELD_SCALES + t : b * FIELD_SCALES + t + 1],
                 )
+
+            planes = transposed.tile([P, WORD * BANK], BF16, tag="words")
+            for e in range(WORD):
+                for i in range(TILES):
+                    nc.tensor.matmul(
+                        out=planes[:, e * N + i * P : e * N + (i + 1) * P],
+                        lhsT=f_rows[b][:, i * D + WORD + e : (i + 1) * D : PLANES],
+                        rhs=identity_bf16[:],
+                        start=True,
+                        stop=True,
+                    )
+            for e in range(WORD):
+                scale_plane(WORD + e, planes[:, e * N : (e + 1) * N])
+            f_words = f_rows[b][:].bitcast(F32)
+            bank = transposed.tile([P, BANK], F32, tag="words")
+            for i in range(TILES):
+                row = i * ROW_WORDS
+                nc.tensor.transpose(bank[:, i * P : (i + 1) * P], f_words[:, row : row + ROW_WORDS : HALVES], identity[:])
+            values = bank[:].bitcast(BF16).rearrange("q (x e) -> q x e", e=WORD)
+            for e in range(WORD):
+                scale_plane(e, values[:, :, e])
 
         def quantise_h(b):
             codes = work.tile([P, N], U32, tag="h_codes", align_bytes=64)
@@ -465,6 +479,14 @@ def tile_fieldinteractionoperators_pa_t_kernel(
         def entry(b):
             return 0 <= b < B
 
+        def transpose_entry_h(b):
+            for pair in range(TILES // BLOCKS_IN_BANK):
+                transpose_h(b, pair)
+
+        def transpose_entry_fields(b):
+            transpose_fields(b)
+            write_last_rows(b)
+
         def step(j):
             if entry(j + LOADS_AHEAD):
                 load_h(j + LOADS_AHEAD)
@@ -475,26 +497,23 @@ def tile_fieldinteractionoperators_pa_t_kernel(
                 first_product_and_fusion(j, i)
             if last:
                 quantise_enhanced(j, slice(N // 2, N))
-            if entry(done):
-                for i in range(TILES // 2):
-                    second_product(done, i, i == OUT_TILE_ON_GPSIMD and not last)
-                store(done, 0, TILES // 2)
+            for i in range(TILES // 2):
+                second_product(done, i, i == OUT_TILE_ON_GPSIMD)
+            store(done, 0, TILES // 2)
             if entry(j + FIELDS_AHEAD):
-                for u in range(HALVES):
-                    transpose_fields(j + FIELDS_AHEAD, u)
-                write_last_rows(j + FIELDS_AHEAD)
+                transpose_entry_fields(j + FIELDS_AHEAD)
             if not last:
                 first_product_and_fusion(j, EARLY_TILES)
-            if entry(done):
-                for i in range(TILES // 2, TILES):
-                    second_product(done, i)
-                store(done, TILES // 2, TILES // 2)
+            for i in range(TILES // 2, TILES):
+                second_product(done, i)
+            store(done, TILES // 2, TILES // 2)
             if entry(j + PREPARED_AHEAD):
                 total_fields(j + PREPARED_AHEAD)
-            for b in range(H_AHEAD - 1 if j == 0 else j + H_AHEAD, j + H_AHEAD + 1):
+            for b in range(H_AHEAD if j == 1 else j + H_AHEAD, j + H_AHEAD + 1):
                 if entry(b):
-                    for pair in range(TILES // BLOCKS_IN_BANK):
-                        transpose_h(b, pair)
+                    transpose_entry_h(b)
+            if j == 1:
+                quantise_h(PREPARED_AHEAD)
             if entry(j + PREPARED_AHEAD):
                 field_scales_products(j + PREPARED_AHEAD)
             quantise_enhanced(j, slice(0, N // 2 if last else N))
@@ -503,33 +522,36 @@ def tile_fieldinteractionoperators_pa_t_kernel(
                 field_scales_sums(j + PREPARED_AHEAD)
                 scale_last_rows(j + PREPARED_AHEAD)
 
-        def transpose_entry_h(b):
-            for pair in range(TILES // BLOCKS_IN_BANK):
-                transpose_h(b, pair)
-
         transpose_entry_h(0)
         total_fields(0)
         base(1)
         field_scales_products(0)
         base(2)
-        nc.vector.tensor_scalar_mul(out=nl_bias[:], in0=b3_planes[:], scalar1=iw[:, 1:2])
         base(3)
-        w3_grouped = weight_to_words(w3_rows)
+        w3_grouped = weight_to_words(w3_rows, nc.scalar.copy)
         field_scales_sums(0)
         scale_last_rows(0)
-        transpose_entry_h(1)
         quantise_h(0)
-        for u in range(HALVES):
-            transpose_fields(0, u)
+        nc.vector.tensor_scalar_mul(out=nl_bias[:], in0=b3_planes[:], scalar1=iw[:, 1:2])
+        transpose_entry_fields(0)
         quantise(w3_grouped, w3_codes, w3_scales)
-        write_last_rows(0)
+        out_w_grouped = weight_to_words(out_w_rows, nc.vector.tensor_copy)
         total_fields(1)
         field_scales_products(1)
-        quantise_h(1)
+        quantise(out_w_grouped, out_w_codes, out_w_scales)
         field_scales_sums(1)
         scale_last_rows(1)
-        quantise(weight_to_words(out_w_rows), out_w_codes, out_w_scales)
-        step(0)
+        for i in range(TILES):
+            first_product_and_fusion(0, i)
+        transpose_entry_h(1)
+        transpose_entry_fields(1)
+        total_fields(2)
+        quantise_h(1)
+        field_scales_products(2)
+        quantise_enhanced(0, slice(0, N))
+        field_scales_sums(2)
+        scale_last_rows(2)
+        transpose_entry_h(2)
         out_bias_ps = products.tile([P, BANK], F32, tag="product")
         nc.tensor.matmul(out=out_bias_ps[:], lhsT=ones[:], rhs=vector_rows[:, 0:D], start=True, stop=True)
         out_bias = const.tile([P, D], F32)

@@ -20,6 +20,7 @@ D = 512
 HEADS = 8
 EDGE_TOKENS = 2
 LAGS = 3
+RUN = 4
 KERNELS = HEADS * LAGS * LAGS
 STREAMS = 2
 INTER_W = 80
@@ -428,9 +429,19 @@ def tile_fieldinteractionoperators_pa_t_kernel(
             field_term = field_terms[b][:].rearrange("q (t i r) -> q i r t", t=PLANES, i=TILES)[:, i]
             if i == FUSION_ON_GPSIMD:
                 weighted = work.tile([P, BANK], F32, tag="weighted")
-                weighted_tile = weighted[:].rearrange("q (r t) -> q r t", t=PLANES)
-                nc.scalar.activation(out=weighted_tile, in_=alternately, func=ACT.Copy, scale=iw[:, 1:2])
-                nc.gpsimd.tensor_tensor(out=fused_tile, in0=weighted_tile, in1=field_term, op=ALU.add)
+                weighted_runs = weighted[:].rearrange("q (c t x) -> q c t x", t=PLANES, x=RUN)
+                nc.scalar.activation(
+                    out=weighted_runs,
+                    in_=nl[:].rearrange("q (t c x) -> q c t x", t=PLANES, x=RUN),
+                    func=ACT.Copy,
+                    scale=iw[:, 1:2],
+                )
+                nc.gpsimd.tensor_tensor(
+                    out=enhanced[b][:, i * BANK : (i + 1) * BANK].rearrange("q (c x t) -> q c t x", t=PLANES, x=RUN),
+                    in0=weighted_runs,
+                    in1=field_terms[b][:].rearrange("q (t i c x) -> q i c t x", t=PLANES, i=TILES, x=RUN)[:, i],
+                    op=ALU.add,
+                )
             else:
                 nc.vector.scalar_tensor_tensor(
                     out=fused_tile, in0=alternately, scalar=iw[:, 1:2], in1=field_term, op0=ALU.mult, op1=ALU.add

from contextlib import ExitStack

import concourse.mybir as mybir
from concourse.masks import make_identity

F32 = mybir.dt.float32
BF16 = mybir.dt.bfloat16
U32 = mybir.dt.uint32
U8 = mybir.dt.uint8
FP8X4 = mybir.dt.float8_e4m3fn_x4
ALU = mybir.AluOpType
ACT = mybir.ActivationFunctionType
AXIS = mybir.AxisListType

P = 128
BANK = 512
B = 16
N = 512
D = 512
HEADS = 8
EDGE_TOKENS = 2
LAGS = 3
RUN = 4
KERNELS = HEADS * LAGS * LAGS
STREAMS = 2
INTER_W = 80
TILES = N // P
PLANES = 4
WORD = 2
HALVES = PLANES // WORD
ROW_WORDS = D // WORD
ROW = TILES * D
BLOCKS_IN_BANK = BANK // (HALVES * P)

KERNEL_CHANNELS = 3
HEAD_PARTITIONS = P // HEADS
SUMS = KERNEL_CHANNELS * HEADS
SCALED_TILES = LAGS
SLOTS = HEADS + 1
BASE = HEADS
TERMS = SCALED_TILES * KERNEL_CHANNELS * SLOTS
FIELD_SCALES = TILES * PLANES

LOADS_AHEAD = 6
H_AHEAD = 3
PREPARED_AHEAD = 2
FIELDS_AHEAD = 1
SECOND_PRODUCT_BEHIND = 1
FUSION_ON_GPSIMD = 0
OUT_TILE_ON_GPSIMD = 0
EARLY_TILES = 3
WORK_BUFFERS = 2
H_BUFFERS = 3
RESULT_BUFFERS = 3
WORD_BANKS = 3
PRODUCT_BANKS = 5

FLOPS = 2 * 2 * B * N * D * D


def tile_fieldinteractionoperators_pa_t_kernel(
    tc, fields, h2, corr_kernels, w3, b3, out_w, out_b, inter_w, out
):
    nc = tc.nc
    with ExitStack() as ctx:
        ctx.enter_context(tc.manual_schedule())
        const = ctx.enter_context(tc.tile_pool(name="const", bufs=1))
        rows_in = ctx.enter_context(tc.tile_pool(name="rows_in", bufs=LOADS_AHEAD + 1))
        work = ctx.enter_context(tc.tile_pool(name="work", bufs=WORK_BUFFERS))
        rows_out = ctx.enter_context(tc.tile_pool(name="rows_out", bufs=RESULT_BUFFERS))
        transposed = ctx.enter_context(tc.psum_pool(name="transposed", bufs=WORD_BANKS))
        products = ctx.enter_context(tc.psum_pool(name="products", bufs=PRODUCT_BANKS))

        identity = const.tile([P, P], F32)
        make_identity(nc, identity[:])
        terms_all = const.tile([P, B * TERMS], F32)

        vector_rows = const.tile([P, D + INTER_W + STREAMS], BF16)
        nc.vector.memset(vector_rows[:], 0.0)
        zero_column = const.tile([P, 1], F32)
        nc.vector.memset(zero_column[:], 0.0)
        edge_rows = const.tile([P, EDGE_TOKENS * D], BF16)
        nc.gpsimd.memset(edge_rows[P // 2 :, :], 0.0)
        ones = const.tile([P, P], BF16)
        nc.vector.memset(ones[:], 1.0)
        scales_all = const.tile([P, B * FIELD_SCALES], F32)
        nc.vector.memset(scales_all[:], 1.0)
        identity_bf16 = const.tile([P, P], BF16)
        nc.vector.tensor_copy(out=identity_bf16[:], in_=identity[:])
        weights = const.tile([P, (LAGS + 2) * SUMS], F32)

        h_rows = {}
        f_rows = {}

        def load_h(b):
            h_tile = rows_in.tile([P, ROW], BF16, tag="h_rows")
            nc.sync.dma_start(out=h_tile[:], in_=h2[b].rearrange("(p i) c -> p (i c)", i=TILES))
            h_rows[b] = h_tile

        def load_fields(b):
            f_tile = rows_in.tile([P, ROW], BF16, tag="f_rows")
            nc.sync.dma_start(out=f_tile[:], in_=fields[b].rearrange("(p i) c -> p (i c)", i=TILES))
            f_rows[b] = f_tile

        for m in range(2 * TILES // EDGE_TOKENS):
            first_token = EDGE_TOKENS * m if m < TILES // EDGE_TOKENS else N - 2 * TILES + EDGE_TOKENS * m
            nc.sync.dma_start(
                out=edge_rows[B * m : B * (m + 1), :],
                in_=fields[:, first_token : first_token + EDGE_TOKENS, :].rearrange("b n c -> b (n c)"),
            )
        nc.sync.dma_start(
            out=vector_rows[0:1, D + INTER_W : D + INTER_W + STREAMS], in_=inter_w.rearrange("(o s) -> o s", o=1)
        )
        nc.sync.dma_start(
            out=vector_rows[0:1, D : D + KERNELS], in_=corr_kernels.rearrange("(o h) l j -> o (h l j)", o=1)
        )
        load_h(0)
        load_fields(0)
        w3_rows = const.tile([P, ROW], BF16)
        nc.sync.dma_start(out=w3_rows[:], in_=w3.rearrange("(m t) k -> m (t k)", t=PLANES))
        b3_planes = const.tile([P, PLANES], BF16)
        nc.sync.dma_start(out=b3_planes[:], in_=b3.rearrange("(q t) -> q t", t=PLANES))
        out_w_rows = const.tile([P, ROW], BF16)
        nc.sync.dma_start(
            out=out_w_rows[:].rearrange("m (a k) -> m a k", a=TILES),
            in_=out_w.rearrange("(a m) k -> m a k", a=TILES),
        )
        nc.sync.dma_start(out=vector_rows[0:1, 0:D], in_=out_b.rearrange("(o c) -> o c", o=1))
        for b in range(1, LOADS_AHEAD + 1):
            load_h(b)
            load_fields(b)

        def rows_to_words(rows, grouped, pair, bank, copy):
            words = rows[:].bitcast(F32)
            grouped_words = grouped[:].bitcast(F32)
            for k in range(BLOCKS_IN_BANK):
                for u in range(HALVES):
                    row = (BLOCKS_IN_BANK * pair + k) * ROW_WORDS
                    nc.tensor.transpose(
                        bank[:, (HALVES * k + u) * P : (HALVES * k + u + 1) * P],
                        words[:, row + u : row + ROW_WORDS : HALVES],
                        identity[:],
                    )
            copy(
                out=grouped_words[:, pair * BANK : (pair + 1) * BANK].rearrange(
                    "q (k r u) -> q k r u", k=BLOCKS_IN_BANK, u=HALVES
                ),
                in_=bank[:].rearrange("q (k u r) -> q k r u", k=BLOCKS_IN_BANK, u=HALVES),
            )

        def quantise(grouped, codes, scales):
            nc.vector.quantize_mx(out=codes[:].bitcast(FP8X4), scales=scales[:], in_=grouped[:])

        def weight_to_words(rows, copy):
            grouped = work.tile([P, PLANES * D], BF16, tag="weight_grouped", align_bytes=64)
            for pair in range(TILES // BLOCKS_IN_BANK):
                bank = products.tile([P, BANK], F32, tag="product")
                rows_to_words(rows, grouped, pair, bank, copy)
            return grouped


        warm = const.tile([P, 1], F32)
        nc.scalar.activation(out=warm[:], in_=zero_column[:], func=ACT.Exp)

        edges = const.tile([P, 2 * TILES * B * PLANES], F32)
        edges_nmbt = edges[:].rearrange("q (n m b t) -> q n m b t", n=EDGE_TOKENS, b=B, t=PLANES)
        edge_words = edge_rows[:].bitcast(F32)
        edge_bank = transposed.tile([P, BANK], F32, tag="words")
        for n in range(EDGE_TOKENS):
            for u in range(HALVES):
                row = n * ROW_WORDS
                nc.tensor.transpose(
                    edge_bank[:, (HALVES * n + u) * P : (HALVES * n + u + 1) * P],
                    edge_words[:, row + u : row + ROW_WORDS : HALVES],
                    identity[:],
                )

        small = products.tile([P, BANK], F32, tag="product")
        nc.tensor.matmul(
            out=small[:, 0 : INTER_W + STREAMS], lhsT=ones[:], rhs=vector_rows[:, D:], start=True, stop=True
        )

        def copy_edges(n):
            edge_values = edge_bank[:].bitcast(BF16).rearrange(
                "q (n u x e) -> q n x u e", n=EDGE_TOKENS, u=HALVES, e=WORD
            )
            nc.vector.tensor_copy(
                out=edges[:].rearrange("q (n x u e) -> q n x u e", n=EDGE_TOKENS, u=HALVES, e=WORD)[:, n],
                in_=edge_values[:, n, 0 : P // 2],
            )

        def token(k):
            return edges_nmbt[:, k % EDGE_TOKENS, k // EDGE_TOKENS, :, 0:KERNEL_CHANNELS]

        heads = const.tile([P, LAGS * B * KERNEL_CHANNELS], F32)
        heads_of_lag = heads[:].rearrange("q (l b j) -> q l b j", l=LAGS, b=B)

        kernels = small[:, 0:KERNELS]
        logits = small[:, INTER_W : INTER_W + STREAMS]
        lives_here = identity[:].rearrange("p (h x) -> p x h", x=HEAD_PARTITIONS)[:, 0:1, :]
        own = weights[:, 2 * SUMS :]

        def own_weight(lag):
            nc.vector.scalar_tensor_tensor(
                out=own[:, (lag - 1) * SUMS : lag * SUMS].rearrange("p (j h) -> p j h", h=HEADS),
                in0=kernels.rearrange("p (h l j) -> p l j h", h=HEADS, l=LAGS)[:, lag - 1],
                scalar=1.0 / (LAGS * (N - lag)),
                in1=lives_here.to_broadcast([P, KERNEL_CHANNELS, HEADS]),
                op0=ALU.mult,
                op1=ALU.mult,
            )

        def add_weight(lag):
            block = LAGS - lag
            nc.vector.tensor_tensor(
                out=weights[:, block * SUMS : (block + 1) * SUMS],
                in0=weights[:, (block + 1) * SUMS : (block + 2) * SUMS],
                in1=weights[:, (lag + 1) * SUMS : (lag + 2) * SUMS],
                op=ALU.add,
            )

        top = const.tile([P, 1], F32)
        nc.vector.tensor_reduce(out=top[:], in_=logits, axis=AXIS.X, op=ALU.max)
        copy_edges(0)
        minus_top = const.tile([P, 1], F32)
        nc.vector.tensor_scalar_mul(out=minus_top[:], in0=top[:], scalar1=-1.0)
        exps = const.tile([P, STREAMS], F32)
        exp_sum = const.tile([P, 1], F32)
        nc.scalar.activation(
            out=exps[:], in_=logits, func=ACT.Exp, bias=minus_top[:, 0:1], scale=1.0, accum_out=exp_sum[:, 0:1]
        )
        copy_edges(1)
        own_weight(1)
        own_weight(2)
        nc.vector.tensor_copy(out=heads_of_lag[:, 0], in_=token(0))
        own_weight(3)
        nc.vector.tensor_tensor(out=heads_of_lag[:, 1], in0=token(0), in1=token(1), op=ALU.add)
        plane_weight = const.tile([P, LAGS * KERNEL_CHANNELS], F32)
        add_weight(2)
        nc.vector.tensor_reduce(
            out=plane_weight[:], in_=own.rearrange("p (x h) -> p x h", h=HEADS), axis=AXIS.X, op=ALU.add
        )
        inv_sum = const.tile([P, 1], F32)
        nc.vector.reciprocal(out=inv_sum[:], in_=exp_sum[:])
        nc.vector.tensor_tensor(out=heads_of_lag[:, 2], in0=heads_of_lag[:, 1], in1=token(2), op=ALU.add)
        add_weight(3)
        iw = const.tile([P, STREAMS], F32)
        nc.vector.tensor_scalar_mul(out=iw[:], in0=exps[:], scalar1=inv_sum[:, 0:1])
        head_terms = const.tile([P, LAGS * B * KERNEL_CHANNELS], F32)
        head_terms_of_lag = head_terms[:].rearrange("q (l b j) -> q l b j", l=LAGS, b=B)
        nc.vector.tensor_tensor(
            out=head_terms_of_lag,
            in0=heads_of_lag,
            in1=plane_weight[:]
            .rearrange("q (l j) -> q l j", l=LAGS)
            .unsqueeze(2)
            .to_broadcast([P, LAGS, B, KERNEL_CHANNELS]),
            op=ALU.mult,
        )
        minus_iw0 = const.tile([P, 1], F32)
        nc.vector.tensor_scalar_mul(out=minus_iw0[:], in0=iw[:, 0:1], scalar1=-1.0)
        total_weight = const.tile([P, SCALED_TILES * SUMS], F32)
        nc.vector.tensor_scalar_mul(out=total_weight[:], in0=weights[:, 0 : SCALED_TILES * SUMS], scalar1=iw[:, 0:1])
        bases = terms_all[:].rearrange("q (b i j s) -> q i b j s", b=B, i=SCALED_TILES, s=SLOTS)[:, :, :, :, BASE]

        def base(lag):
            i = LAGS - lag
            if lag == 1:
                nc.vector.tensor_scalar(
                    out=bases[:, i],
                    in0=head_terms_of_lag[:, 0],
                    scalar1=minus_iw0[:, 0:1],
                    scalar2=1.0,
                    op0=ALU.mult,
                    op1=ALU.add,
                )
            else:
                nc.vector.scalar_tensor_tensor(
                    out=bases[:, i],
                    in0=head_terms_of_lag[:, lag - 1],
                    scalar=minus_iw0[:, 0:1],
                    in1=bases[:, i + 1],
                    op0=ALU.mult,
                    op1=ALU.add,
                )

        nl_bias = const.tile([P, PLANES], F32)
        w3_codes = const.tile([P, D], U32, align_bytes=64)
        w3_scales = const.tile([P, D], U8, align_bytes=64)

        h_grouped = {}
        h_codes = {}
        h_scales = {}
        field_totals = {}
        field_terms = {}
        last_scaled = {}
        enhanced = {}
        e_codes = {}
        e_scales = {}
        results = {}
        out_w_codes = const.tile([P, D], U32, align_bytes=64)
        out_w_scales = const.tile([P, D], U8, align_bytes=64)

        def total_fields(b):
            bank = products.tile([P, BANK], F32, tag="product")
            total = bank[:, 0:SUMS]
            kernel_channels = f_rows[b][:].rearrange("p (i h x) -> p i x h", i=TILES, h=HEADS)[:, :, 0:KERNEL_CHANNELS, :]
            for i in range(TILES):
                nc.tensor.matmul(
                    out=total.rearrange("p (j h) -> p j h", h=HEADS),
                    lhsT=ones[:],
                    rhs=kernel_channels[:, i],
                    start=(i == 0),
                    stop=(i == TILES - 1),
                )
            field_totals[b] = total

        def entry_terms(b):
            return terms_all[:, b * TERMS : (b + 1) * TERMS]

        def field_scales_products(b):
            nc.vector.tensor_tensor(
                out=entry_terms(b).rearrange("q (i c s) -> q i c s", i=SCALED_TILES, s=SLOTS)[:, :, :, 0:HEADS],
                in0=field_totals[b]
                .rearrange("q (c h) -> q c h", h=HEADS)
                .unsqueeze(1)
                .to_broadcast([P, SCALED_TILES, KERNEL_CHANNELS, HEADS]),
                in1=total_weight[:].rearrange("q (i c h) -> q i c h", i=SCALED_TILES, h=HEADS),
                op=ALU.mult,
            )

        def field_scales_sums(b):
            nc.vector.tensor_reduce(
                out=scales_all[:, b * FIELD_SCALES : (b + 1) * FIELD_SCALES].rearrange("q (i t) -> q i t", t=PLANES)[
                    :, 0:SCALED_TILES, 0:KERNEL_CHANNELS
                ],
                in_=entry_terms(b).rearrange("q (i c s) -> q i c s", i=SCALED_TILES, s=SLOTS),
                axis=AXIS.X,
                op=ALU.add,
            )

        def scale_last_rows(b):
            scaled = work.tile([P, FIELD_SCALES], F32, tag="last_scaled")
            nc.gpsimd.tensor_tensor(
                out=scaled[:].rearrange("q (m n t) -> q m n t", n=EDGE_TOKENS, t=PLANES),
                in0=edges_nmbt[:, :, TILES // EDGE_TOKENS :, b, :].rearrange("q n m t -> q m n t"),
                in1=scales_all[:, b * FIELD_SCALES : (b + 1) * FIELD_SCALES].rearrange(
                    "q (m n t) -> q m n t", n=EDGE_TOKENS, t=PLANES
                ),
                op=ALU.mult,
            )
            last_scaled[b] = scaled

        def write_last_rows(b):
            nc.gpsimd.tensor_tensor(
                out=field_terms[b][:].rearrange("q (t i r) -> q i t r", t=PLANES, i=TILES)[:, :, :, P - 1],
                in0=last_scaled[b][:].rearrange("q (i t) -> q i t", i=TILES),
                in1=nl_bias[:].unsqueeze(1).to_broadcast([P, TILES, PLANES]),
                op=ALU.add,
            )

        def transpose_h(b, pair):
            if pair == 0:
                grouped = work.tile([P, PLANES * N], BF16, tag="h_grouped", bufs=H_BUFFERS, align_bytes=64)
                h_grouped[b] = grouped
            bank = transposed.tile([P, BANK], F32, tag="words")
            rows_to_words(h_rows[b], h_grouped[b], pair, bank, nc.scalar.copy)

        def transpose_fields(b):
            term = work.tile([P, PLANES * N], F32, tag="field_term")
            field_terms[b] = term

            def scale_plane(t, values):
                nc.scalar.activation(
                    out=field_terms[b][:, t * N : (t + 1) * N],
                    in_=values,
                    func=ACT.Identity,
                    bias=nl_bias[:, t : t + 1],
                    scale=scales_all[:, b * FIELD_SCALES + t : b * FIELD_SCALES + t + 1],
                )

            planes = transposed.tile([P, WORD * BANK], BF16, tag="words")
            for e in range(WORD):
                for i in range(TILES):
                    nc.tensor.matmul(
                        out=planes[:, e * N + i * P : e * N + (i + 1) * P],
                        lhsT=f_rows[b][:, i * D + WORD + e : (i + 1) * D : PLANES],
                        rhs=identity_bf16[:],
                        start=True,
                        stop=True,
                    )
            for e in range(WORD):
                scale_plane(WORD + e, planes[:, e * N : (e + 1) * N])
            f_words = f_rows[b][:].bitcast(F32)
            bank = transposed.tile([P, BANK], F32, tag="words")
            for i in range(TILES):
                row = i * ROW_WORDS
                nc.tensor.transpose(bank[:, i * P : (i + 1) * P], f_words[:, row : row + ROW_WORDS : HALVES], identity[:])
            values = bank[:].bitcast(BF16).rearrange("q (x e) -> q x e", e=WORD)
            for e in range(WORD):
                scale_plane(e, values[:, :, e])

        def quantise_h(b):
            codes = work.tile([P, N], U32, tag="h_codes", align_bytes=64)
            scales = work.tile([P, N], U8, tag="h_scales", align_bytes=64)
            quantise(h_grouped[b], codes, scales)
            h_codes[b] = codes
            h_scales[b] = scales

        def first_product_and_fusion(b, i):
            if i == 0:
                fused = work.tile([P, PLANES * N], BF16, tag="enhanced", align_bytes=64)
                enhanced[b] = fused
            tokens = slice(i * P, (i + 1) * P)
            nl = products.tile([P, BANK], F32, tag="product")
            for t in range(PLANES):
                channels = slice(t * P, (t + 1) * P)
                nc.tensor.matmul_mx(
                    out=nl[:, channels],
                    lhsT=w3_codes[:, channels].bitcast(FP8X4),
                    lhsT_scale=w3_scales[:, channels],
                    rhs=h_codes[b][:, tokens].bitcast(FP8X4),
                    rhs_scale=h_scales[b][:, tokens],
                    start=True,
                    stop=True,
                )
            alternately = nl[:].rearrange("q (t r) -> q r t", t=PLANES)
            fused_tile = enhanced[b][:, i * BANK : (i + 1) * BANK].rearrange("q (r t) -> q r t", t=PLANES)
            field_term = field_terms[b][:].rearrange("q (t i r) -> q i r t", t=PLANES, i=TILES)[:, i]
            if i == FUSION_ON_GPSIMD:
                weighted = work.tile([P, BANK], F32, tag="weighted")
                weighted_runs = weighted[:].rearrange("q (c t x) -> q c t x", t=PLANES, x=RUN)
                nc.scalar.activation(
                    out=weighted_runs,
                    in_=nl[:].rearrange("q (t c x) -> q c t x", t=PLANES, x=RUN),
                    func=ACT.Copy,
                    scale=iw[:, 1:2],
                )
                nc.gpsimd.tensor_tensor(
                    out=enhanced[b][:, i * BANK : (i + 1) * BANK].rearrange("q (c x t) -> q c t x", t=PLANES, x=RUN),
                    in0=weighted_runs,
                    in1=field_terms[b][:].rearrange("q (t i c x) -> q i c t x", t=PLANES, i=TILES, x=RUN)[:, i],
                    op=ALU.add,
                )
            else:
                nc.vector.scalar_tensor_tensor(
                    out=fused_tile, in0=alternately, scalar=iw[:, 1:2], in1=field_term, op0=ALU.mult, op1=ALU.add
                )

        def quantise_enhanced(b, tokens):
            if b not in e_codes:
                codes = work.tile([P, N], U32, tag="e_codes", align_bytes=64)
                scales = work.tile([P, N], U8, tag="e_scales", align_bytes=64)
                e_codes[b] = codes
                e_scales[b] = scales
            nc.vector.quantize_mx(
                out=e_codes[b][:, tokens].bitcast(FP8X4),
                scales=e_scales[b][:, tokens],
                in_=enhanced[b][:, PLANES * tokens.start : PLANES * tokens.stop],
            )

        def second_product(b, i, on_gpsimd=False):
            if b not in results:
                result = rows_out.tile([P, TILES * D], F32, tag="result")
                results[b] = result
            tokens = slice(i * P, (i + 1) * P)
            columns = slice(i * D, (i + 1) * D)
            projected = products.tile([P, BANK], F32, tag="product")
            nc.tensor.matmul_mx(
                out=projected[:],
                lhsT=e_codes[b][:, tokens].bitcast(FP8X4),
                lhsT_scale=e_scales[b][:, tokens],
                rhs=out_w_codes[:].bitcast(FP8X4),
                rhs_scale=out_w_scales[:],
                start=True,
                stop=True,
            )
            if on_gpsimd:
                nc.scalar.copy(out=results[b][:, columns], in_=projected[:])
                nc.gpsimd.tensor_tensor(
                    out=results[b][:, columns], in0=results[b][:, columns], in1=out_bias[:], op=ALU.add
                )
            else:
                nc.vector.tensor_tensor(out=results[b][:, columns], in0=projected[:], in1=out_bias[:], op=ALU.add)

        def store(b, first, tiles):
            run = slice(first * D, (first + tiles) * D)
            nc.sync.dma_start(out=out[b].rearrange("(p i) o -> p (i o)", i=TILES)[:, run], in_=results[b][:, run])

        def entry(b):
            return 0 <= b < B

        def transpose_entry_h(b):
            for pair in range(TILES // BLOCKS_IN_BANK):
                transpose_h(b, pair)

        def transpose_entry_fields(b):
            transpose_fields(b)
            write_last_rows(b)

        def step(j):
            if entry(j + LOADS_AHEAD):
                load_h(j + LOADS_AHEAD)
                load_fields(j + LOADS_AHEAD)
            done = j - SECOND_PRODUCT_BEHIND
            last = j == B - 1
            for i in range(TILES if last else EARLY_TILES):
                first_product_and_fusion(j, i)
            if last:
                quantise_enhanced(j, slice(N // 2, N))
            for i in range(TILES // 2):
                second_product(done, i, i == OUT_TILE_ON_GPSIMD)
            store(done, 0, TILES // 2)
            if entry(j + FIELDS_AHEAD):
                transpose_entry_fields(j + FIELDS_AHEAD)
            if not last:
                first_product_and_fusion(j, EARLY_TILES)
            for i in range(TILES // 2, TILES):
                second_product(done, i)
            store(done, TILES // 2, TILES // 2)
            if entry(j + PREPARED_AHEAD):
                total_fields(j + PREPARED_AHEAD)
            for b in range(H_AHEAD if j == 1 else j + H_AHEAD, j + H_AHEAD + 1):
                if entry(b):
                    transpose_entry_h(b)
            if j == 1:
                quantise_h(PREPARED_AHEAD)
            if entry(j + PREPARED_AHEAD):
                field_scales_products(j + PREPARED_AHEAD)
            quantise_enhanced(j, slice(0, N // 2 if last else N))
            if entry(j + PREPARED_AHEAD):
                quantise_h(j + PREPARED_AHEAD)
                field_scales_sums(j + PREPARED_AHEAD)
                scale_last_rows(j + PREPARED_AHEAD)

        transpose_entry_h(0)
        total_fields(0)
        base(1)
        field_scales_products(0)
        base(2)
        base(3)
        w3_grouped = weight_to_words(w3_rows, nc.scalar.copy)
        field_scales_sums(0)
        scale_last_rows(0)
        quantise_h(0)
        nc.vector.tensor_scalar_mul(out=nl_bias[:], in0=b3_planes[:], scalar1=iw[:, 1:2])
        transpose_entry_fields(0)
        quantise(w3_grouped, w3_codes, w3_scales)
        out_w_grouped = weight_to_words(out_w_rows, nc.vector.tensor_copy)
        total_fields(1)
        field_scales_products(1)
        quantise(out_w_grouped, out_w_codes, out_w_scales)
        field_scales_sums(1)
        scale_last_rows(1)
        for i in range(TILES):
            first_product_and_fusion(0, i)
        transpose_entry_h(1)
        transpose_entry_fields(1)
        total_fields(2)
        quantise_h(1)
        field_scales_products(2)
        quantise_enhanced(0, slice(0, N))
        field_scales_sums(2)
        scale_last_rows(2)
        transpose_entry_h(2)
        out_bias_ps = products.tile([P, BANK], F32, tag="product")
        nc.tensor.matmul(out=out_bias_ps[:], lhsT=ones[:], rhs=vector_rows[:, 0:D], start=True, stop=True)
        out_bias = const.tile([P, D], F32)
        nc.scalar.copy(out=out_bias[:], in_=out_bias_ps[:])
        for j in range(1, B):
            step(j)
        for i in [*range(TILES // 2, TILES), *range(TILES // 2)]:
            second_product(B - 1, i)
            store(B - 1, i, 1)
